import numpy as np
import ml_dtypes


def mxq(x, axis, fmt="e4m3"):
    dtype, down = {"e4m3": (ml_dtypes.float8_e4m3fn, 7), "e5m2": (ml_dtypes.float8_e5m2, 14)}[fmt]
    v = np.moveaxis(np.asarray(x, np.float32).astype(ml_dtypes.bfloat16).astype(np.float64), axis, -1)
    blocks = v.reshape(v.shape[:-1] + (-1, 32))
    amax = np.abs(blocks).max(-1, keepdims=True)
    byte = np.maximum(np.where(amax > 0, np.frexp(amax)[1] - 1 + 127, 0) - down, 1)
    scale = np.exp2(byte - 127.0)
    codes = (blocks / scale).astype(np.float32).astype(dtype).astype(np.float64)
    return np.moveaxis((codes * scale).reshape(v.shape), -1, axis)


WIDE = False


def mx_kscale(k):
    if not WIDE:
        return np.ones(k)
    levels = np.array([10, -10, 5, -5, 0])
    a = np.random.permutation(np.resize(levels, k // 512 * 4)).reshape(k // 512, 4)
    idx = np.arange(k)
    return np.exp2(a[idx // 512, idx % 128 // 32])


BF16 = ml_dtypes.bfloat16


def bf(x):
    return np.asarray(x, np.float32).astype(BF16)


def f64(x):
    return np.asarray(x).astype(np.float64)


E2M1 = np.array([0.0, 0.5, 1.0, 1.5, 2.0, 3.0, 4.0, 6.0, -0.0, -0.5, -1.0, -1.5, -2.0, -3.0, -4.0, -6.0])


def pack_weight(w, fmt):
    k, n = w.shape
    w = f64(bf(w)).reshape(k // 32, 32, n)
    amax = np.abs(w).max(1)
    if fmt == "e4m3":
        byte = np.frexp(amax)[1] - 1 + 127 - 7
    else:
        mant, ex = np.frexp(amax / 6.0)
        byte = np.where(mant > 0.5, ex, ex - 1) + 127
    byte = np.clip(np.where(amax > 0, byte, 1), 1, 254)
    scaled = (w * np.exp2(127.0 - byte)[:, None, :]).reshape(k, n).astype(np.float32)
    by_word = np.ascontiguousarray(scaled.reshape(k // 512, 128, 4, n).transpose(0, 1, 3, 2))
    if fmt == "e4m3":
        words = by_word.astype(ml_dtypes.float8_e4m3fn).view(np.uint8)
    else:
        c = by_word.astype(ml_dtypes.float4_e2m1fn).view(np.uint8) & 0xF
        words = c[..., 0::2] | (c[..., 1::2] << 4)
    return np.ascontiguousarray(words), np.ascontiguousarray(byte.astype(np.uint8).reshape(k // 512, 16, n))


def unpack_weight(words, scales, fmt):
    g, p, n, _ = words.shape
    if fmt == "e4m3":
        vals = np.ascontiguousarray(words).view(ml_dtypes.float8_e4m3fn).astype(np.float64)
    else:
        nib = np.empty((g, p, n, 4), np.uint8)
        nib[..., 0::2] = words & 0xF
        nib[..., 1::2] = words >> 4
        vals = E2M1[nib]
    vals = vals * np.repeat(np.exp2(scales.astype(np.float64) - 127.0), 8, axis=1)[..., None]
    return vals.transpose(0, 1, 3, 2).reshape(g * 512, n)


B, T, STOCH, ACT, HID, DETER, G = 4, 64, 1024, 512, 2560, 1536, 3
N = B * T
BH = DETER // G
BLK_IN = BH + 3 * HID
EPS = 1e-3
FMT = "e4m3"


def silu(v):
    return v / (1.0 + np.exp(-v))


def ln(v, g, b):
    mu = v.mean(-1, keepdims=True)
    var = v.var(-1, keepdims=True)
    return (v - mu) / np.sqrt(var + EPS) * g + b


def setup_inputs():
    ss, sa, sd = mx_kscale(STOCH), mx_kscale(ACT), mx_kscale(DETER)
    w_hid = np.random.standard_normal((G, BLK_IN, BH)) * 0.2 / np.sqrt(BLK_IN)
    w_hid[:, :BH] = w_hid[:, :BH] / sd.reshape(G, BH)[:, :, None]
    s = bf(np.random.standard_normal((B, T, STOCH)) * ss)
    a = bf(np.random.standard_normal((B, T, ACT)) * sa)
    d = bf(np.random.standard_normal((B, T, DETER)) * sd)
    W_s_words, W_s_scales = pack_weight(np.random.standard_normal((STOCH, HID)) * 0.15 / np.sqrt(STOCH) / ss[:, None], FMT)
    W_a_words, W_a_scales = pack_weight(np.random.standard_normal((ACT, HID)) * 0.15 / np.sqrt(ACT) / sa[:, None], FMT)
    W_d_words, W_d_scales = pack_weight(np.random.standard_normal((DETER, HID)) * 0.15 / np.sqrt(DETER) / sd[:, None], FMT)
    return {
        "s": s,
        "a": a,
        "d": d,
        "W_s_words": W_s_words,
        "W_s_scales": W_s_scales,
        "W_a_words": W_a_words,
        "W_a_scales": W_a_scales,
        "W_d_words": W_d_words,
        "W_d_scales": W_d_scales,
        "ln_s_g": bf(1.0 + 0.1 * np.random.standard_normal(HID)),
        "ln_s_b": bf(0.2 * np.random.standard_normal(HID)),
        "ln_a_g": bf(1.0 + 0.1 * np.random.standard_normal(HID)),
        "ln_a_b": bf(0.2 * np.random.standard_normal(HID)),
        "ln_d_g": bf(1.0 + 0.1 * np.random.standard_normal(HID)),
        "ln_d_b": bf(0.2 * np.random.standard_normal(HID)),
        "W_hid": bf(w_hid),
        "ln_h_g": bf(1.0 + 0.1 * np.random.standard_normal(DETER)),
        "ln_h_b": bf(0.2 * np.random.standard_normal(DETER)),
    }


def reference(s, a, d, W_s_words, W_s_scales, W_a_words, W_a_scales, W_d_words, W_d_scales, ln_s_g, ln_s_b, ln_a_g, ln_a_b, ln_d_g, ln_d_b, W_hid, ln_h_g, ln_h_b):
    sq = mxq(f64(s).reshape(N, STOCH), 1, "e4m3")
    aq = mxq(f64(a).reshape(N, ACT), 1, "e4m3")
    dq = mxq(f64(d).reshape(N, DETER), 1, "e4m3")
    s_h = silu(ln(sq @ unpack_weight(W_s_words, W_s_scales, FMT), f64(ln_s_g), f64(ln_s_b)))
    a_h = silu(ln(aq @ unpack_weight(W_a_words, W_a_scales, FMT), f64(ln_a_g), f64(ln_a_b)))
    d_h = silu(ln(dq @ unpack_weight(W_d_words, W_d_scales, FMT), f64(ln_d_g), f64(ln_d_b)))
    xq = mxq(np.concatenate([s_h, a_h, d_h], axis=-1), 1, "e4m3")
    wq = mxq(f64(W_hid), 1, "e4m3")
    p = (dq.reshape(N, G, BH).transpose(1, 0, 2) @ wq[:, :BH]) + (xq @ wq[:, BH:])
    p = p.transpose(1, 0, 2).reshape(N, DETER)
    return silu(ln(p, f64(ln_h_g), f64(ln_h_b)))

@@ -1,0 +1,329 @@
+from contextlib import ExitStack
+
+import concourse.mybir as mybir
+from concourse.masks import make_identity
+
+F32 = mybir.dt.float32
+BF16 = mybir.dt.bfloat16
+I32 = mybir.dt.int32
+U32 = mybir.dt.uint32
+U8 = mybir.dt.uint8
+FP8X4 = mybir.dt.float8_e4m3fn_x4
+ACT = mybir.ActivationFunctionType
+ALU = mybir.AluOpType
+
+P = 128
+PACK = 4
+K_PASS = P * PACK
+BANK = 512
+ROWS = 256
+M_TILES = ROWS // P
+HID = 2560
+HID_BANKS = HID // BANK
+DETER = 1536
+BLOCKS = 3
+BLK = DETER // BLOCKS
+HID_PASSES = 1 + 3 * HID // K_PASS
+EPS = 1e-3
+
+FLOPS = 2 * ROWS * ((1024 + 512 + 1536) * HID + BLOCKS * HID_PASSES * K_PASS * BLK)
+
+
+def regroup(copy, grouped, planes):
+    copy(
+        out=grouped.rearrange("p (c i) t -> p c t i", i=4),
+        in_=planes.rearrange("p t (c i) -> p c t i", i=4),
+    )
+
+
+def norm_scalars(nc, small, banks, neg_half):
+    stats = small.tile([P, len(banks), 6], F32, name="stats", tag="stats%d" % len(banks))
+    for j, bank in enumerate(banks):
+        nc.vector.bn_stats(out=stats[:, j, :], in_=bank[:])
+    mean_var = small.tile([P, 2], F32, name="mean_var")
+    nc.vector.bn_aggr(out=mean_var[:], in_=stats[:].rearrange("p a b -> p (a b)"))
+    var_eps = small.tile([P, 1], F32, name="var_eps")
+    nc.vector.tensor_scalar_add(out=var_eps[:], in0=mean_var[:, 1:2], scalar1=EPS)
+    rstd = small.tile([P, 1], F32, name="rstd")
+    nc.gpsimd.tensor_tensor(out=rstd[:], in0=var_eps[:], in1=neg_half[:], op=ALU.pow)
+    return mean_var, rstd
+
+
+def tile_blockrecurrentmodel_pa_k_kernel(
+    tc,
+    s,
+    a,
+    d,
+    W_s_words,
+    W_s_scales,
+    W_a_words,
+    W_a_scales,
+    W_d_words,
+    W_d_scales,
+    ln_s_g,
+    ln_s_b,
+    ln_a_g,
+    ln_a_b,
+    ln_d_g,
+    ln_d_b,
+    W_hid,
+    ln_h_g,
+    ln_h_b,
+    out,
+):
+    nc = tc.nc
+    with ExitStack() as whole:
+        consts = whole.enter_context(tc.tile_pool(name="consts", bufs=1))
+        small = whole.enter_context(tc.tile_pool(name="small", bufs=4))
+        w_raw_pool = whole.enter_context(tc.tile_pool(name="w_raw", bufs=5))
+        w_grouped_pool = whole.enter_context(tc.tile_pool(name="w_grouped", bufs=3))
+        w_codes_pool = whole.enter_context(tc.tile_pool(name="w_codes", bufs=12))
+        psum_bank = whole.enter_context(tc.psum_pool(name="psum_bank", bufs=6))
+        psum_tr = whole.enter_context(tc.psum_pool(name="psum_tr", bufs=2))
+
+        ident = consts.tile([P, P], F32, name="ident")
+        make_identity(nc, ident[:])
+        ones = consts.tile([P, P], BF16, name="ones")
+        nc.gpsimd.memset(ones[:], 1.0)
+        neg_half = consts.tile([P, 1], F32, name="neg_half")
+        nc.gpsimd.memset(neg_half[:], -0.5)
+        warm = consts.tile([P, 1], F32, name="warm")
+        nc.scalar.activation(out=warm[:], in_=neg_half[:], func=ACT.Silu)
+
+        in_codes = consts.tile([P, 6, ROWS], U32, name="in_codes", align_bytes=64)
+        in_planes = consts.tile([P, 6, ROWS], U8, name="in_planes", align_bytes=64)
+        x_codes = consts.tile([P, 15, ROWS], U32, name="x_codes", align_bytes=64)
+        x_planes = consts.tile([P, 15, ROWS], U8, name="x_planes", align_bytes=64)
+        gain_bias = consts.tile([P, PACK, P], F32, name="gain_bias")
+        out_gain_bias = consts.tile([P, 2 * DETER], BF16, name="out_gain_bias")
+
+        def load_w_hid_pair(pair):
+            block = pair % BLOCKS
+            first_row = (pair // BLOCKS) * 2 * K_PASS
+            raw = w_raw_pool.tile([P, 2, PACK, BLK], BF16, name="w_raw")
+            nc.sync.dma_start(
+                out=raw[:],
+                in_=W_hid[block, first_row : first_row + 2 * K_PASS, :].rearrange(
+                    "(c p t) n -> p c t n", c=2, t=PACK
+                ),
+            )
+            return raw
+
+        w_raw = []
+
+        with ExitStack() as stage1:
+            setup = stage1.enter_context(tc.tile_pool(name="setup", bufs=1))
+            in_grouped_pool = stage1.enter_context(tc.tile_pool(name="in_grouped", bufs=2))
+            w1_pool = stage1.enter_context(tc.tile_pool(name="w1", bufs=4))
+            u_pool = stage1.enter_context(tc.tile_pool(name="u", bufs=16))
+            xt_pool = stage1.enter_context(tc.tile_pool(name="xt", bufs=2))
+
+            planes_sa = setup.tile([P, HID], U8, name="planes_sa", align_bytes=64)
+            planes_d = setup.tile([P, HID], U8, name="planes_d", align_bytes=64)
+            vec_rows = setup.tile([P, K_PASS], BF16, name="vec_rows")
+            out_vec_row = setup.tile([P, 2 * DETER], BF16, name="out_vec_row")
+            nc.vector.memset(planes_sa[:].bitcast(I32), 0)
+            nc.vector.memset(planes_d[:].bitcast(I32), 0)
+            nc.vector.memset(vec_rows[:], 0.0)
+            nc.vector.memset(out_vec_row[:], 0.0)
+
+            streams = [
+                dict(x=a, k=512, words=W_a_words, first_group=2, planes=planes_sa, plane_row=8,
+                     gain_row=10, bias_row=15, first_pass=5),
+                dict(x=s, k=1024, words=W_s_words, first_group=0, planes=planes_sa, plane_row=0,
+                     gain_row=0, bias_row=5, first_pass=0),
+                dict(x=d, k=1536, words=W_d_words, first_group=3, planes=planes_d, plane_row=0,
+                     gain_row=20, bias_row=25, first_pass=10),
+            ]
+
+            for st in streams:
+                x_sb = setup.tile([P, M_TILES, st["k"]], BF16, name="x_sb%d" % st["k"])
+                nc.sync.dma_start(
+                    out=x_sb[:],
+                    in_=st["x"].flatten_outer_dims().rearrange("(m p) k -> p m k", p=P),
+                )
+                st["x_sb"] = x_sb
+            for quad in range(4):
+                rows = slice(4 * quad, 4 * quad + 4)
+                nc.sync.dma_start(
+                    out=planes_sa[32 * quad + 8 : 32 * quad + 12, :].bitcast(I32),
+                    in_=W_a_scales[0, rows, :].bitcast(I32),
+                )
+                nc.sync.dma_start(
+                    out=planes_sa[32 * quad : 32 * quad + 8, :].bitcast(I32),
+                    in_=W_s_scales[:, rows, :].bitcast(I32),
+                )
+                nc.sync.dma_start(
+                    out=planes_d[32 * quad : 32 * quad + 12, :].bitcast(I32),
+                    in_=W_d_scales[:, rows, :].bitcast(I32),
+                )
+            for i, st in enumerate(streams):
+                st["w"] = []
+                for g in range(st["k"] // K_PASS):
+                    w = w1_pool.tile([P, HID], U32, name="w1", align_bytes=64)
+                    nc.sync.dma_start(
+                        out=w[:].bitcast(I32),
+                        in_=st["words"][g].rearrange("p n t -> p (n t)").bitcast(I32),
+                    )
+                    st["w"].append(w)
+                if i == 0:
+                    for v, vec in enumerate([ln_s_g, ln_s_b, ln_a_g, ln_a_b, ln_d_g, ln_d_b]):
+                        nc.sync.dma_start(
+                            out=vec_rows[HID_BANKS * v : HID_BANKS * (v + 1), :],
+                            in_=vec.rearrange("(c k) -> c k", k=K_PASS),
+                        )
+                if i < 2:
+                    w_raw.append(load_w_hid_pair(len(w_raw)))
+                    w_raw.append(load_w_hid_pair(len(w_raw)))
+            nc.sync.dma_start(out=out_vec_row[0:1, 0:DETER], in_=ln_h_g.rearrange("(o k) -> o k", o=1))
+            nc.sync.dma_start(out=out_vec_row[0:1, DETER:], in_=ln_h_b.rearrange("(o k) -> o k", o=1))
+
+            for st in streams:
+                for g in range(st["k"] // K_PASS):
+                    group = st["first_group"] + g
+                    xt = psum_tr.tile([P, 2, ROWS], F32, name="xt_ps", tag="tr")
+                    for half in range(2):
+                        for m in range(M_TILES):
+                            words = st["x_sb"][:, m, :].bitcast(F32)
+                            nc.tensor.transpose(
+                                xt[:, half, m * P : (m + 1) * P],
+                                words[:, 256 * g + half : 256 * (g + 1) : 2],
+                                ident[:],
+                            )
+                    grouped = in_grouped_pool.tile([P, ROWS * PACK], BF16, name="in_grouped", align_bytes=64)
+                    nc.scalar.copy(
+                        out=grouped[:].bitcast(F32).rearrange("p (r h) -> p r h", h=2),
+                        in_=xt[:].rearrange("p h r -> p r h"),
+                    )
+                    nc.vector.quantize_mx(
+                        out=in_codes[:, group, :].bitcast(FP8X4),
+                        scales=in_planes[:, group, :],
+                        in_=grouped[:],
+                    )
+
+            vec_sorted = setup.tile([P, PACK, P], F32, name="vec_sorted")
+            nc.vector.tensor_copy(out=vec_sorted[:], in_=vec_rows[:].rearrange("r (q t) -> r t q", t=PACK))
+            gb_ps = psum_tr.tile([P, PACK, P], F32, name="gb_ps", tag="tr")
+            for t in range(PACK):
+                nc.tensor.transpose(gb_ps[:, t, :], vec_sorted[:, t, :], ident[:])
+            nc.vector.tensor_copy(out=gain_bias[:], in_=gb_ps[:])
+
+            for st in streams:
+                groups = st["k"] // K_PASS
+                u = []
+                for m in range(M_TILES):
+                    m_cols = slice(m * P, (m + 1) * P)
+                    h = []
+                    for j in range(HID_BANKS):
+                        n_cols = slice(j * BANK, (j + 1) * BANK)
+                        bank = psum_bank.tile([P, BANK], F32, name="h", tag="bank")
+                        for g in range(groups):
+                            group = st["first_group"] + g
+                            nc.tensor.matmul_mx(
+                                out=bank[:],
+                                lhsT=in_codes[:, group, m_cols].bitcast(FP8X4),
+                                lhsT_scale=in_planes[:, group, m_cols],
+                                rhs=st["w"][g][:, n_cols].bitcast(FP8X4),
+                                rhs_scale=st["planes"][st["plane_row"] + 4 * g : P, n_cols],
+                                start=(g == 0),
+                                stop=(g == groups - 1),
+                            )
+                        h.append(bank)
+                    mean_var, rstd = norm_scalars(nc, small, h, neg_half)
+                    neg_mean = small.tile([P, 1], F32, name="neg_mean")
+                    nc.vector.tensor_scalar_mul(out=neg_mean[:], in0=mean_var[:, 0:1], scalar1=-1.0)
+                    shift = small.tile([P, 1], F32, name="shift")
+                    nc.gpsimd.tensor_tensor(out=shift[:], in0=neg_mean[:], in1=rstd[:], op=ALU.mult)
+                    u_m = []
+                    for j in range(HID_BANKS):
+                        u_bank = u_pool.tile([P, PACK, P], F32, name="u")
+                        nc.scalar.activation(
+                            out=u_bank[:],
+                            in_=h[j][:].rearrange("p (q t) -> p t q", t=PACK),
+                            func=ACT.Identity,
+                            scale=rstd[:],
+                            bias=shift[:],
+                        )
+                        u_m.append(u_bank)
+                    u.append(u_m)
+
+                for j in range(HID_BANKS):
+                    x_t = xt_pool.tile([P, PACK, ROWS], BF16, name="x_t")
+                    for half in range(2):
+                        z_ps = psum_tr.tile([P, 2, ROWS], F32, name="z_ps", tag="tr")
+                        for i in range(2):
+                            for m in range(M_TILES):
+                                nc.tensor.transpose(
+                                    z_ps[:, i, m * P : (m + 1) * P], u[m][j][:, 2 * half + i, :], ident[:]
+                                )
+                        for i in range(2):
+                            t = 2 * half + i
+                            nc.scalar.activation(
+                                out=x_t[:, t, :],
+                                in_=z_ps[:, i, :],
+                                func=ACT.Silu,
+                                scale=gain_bias[:, t, st["gain_row"] + j : st["gain_row"] + j + 1],
+                                bias=gain_bias[:, t, st["bias_row"] + j : st["bias_row"] + j + 1],
+                            )
+                    x_grouped = xt_pool.tile([P, ROWS, PACK], BF16, name="x_grouped", align_bytes=64)
+                    regroup(nc.vector.tensor_copy, x_grouped[:], x_t[:])
+                    nc.vector.quantize_mx(
+                        out=x_codes[:, st["first_pass"] + j, :].bitcast(FP8X4),
+                        scales=x_planes[:, st["first_pass"] + j, :],
+                        in_=x_grouped[:].rearrange("p n t -> p (n t)"),
+                    )
+
+            for j in range(2 * DETER // BANK):
+                n_cols = slice(j * BANK, (j + 1) * BANK)
+                spread = psum_tr.tile([P, BANK], F32, name="spread", tag="tr")
+                nc.tensor.matmul(out=spread[:], lhsT=ones[:], rhs=out_vec_row[:, n_cols], start=True, stop=True)
+                nc.scalar.copy(out=out_gain_bias[:, n_cols], in_=spread[:])
+
+        acc = [[psum_bank.tile([P, BANK], F32, name="acc", tag="bank") for m in range(M_TILES)] for g in range(BLOCKS)]
+        for pair in range(BLOCKS * HID_PASSES // 2):
+            if pair >= len(w_raw):
+                w_raw.append(load_w_hid_pair(pair))
+            block = pair % BLOCKS
+            for c in range(2):
+                k_pass = (pair // BLOCKS) * 2 + c
+                grouped = w_grouped_pool.tile([P, BLK, PACK], BF16, name="w_grouped", align_bytes=64)
+                regroup(nc.vector.tensor_copy if c == 0 else nc.scalar.copy, grouped[:], w_raw[pair][:, c, :, :])
+                codes = w_codes_pool.tile([P, BLK], U32, name="w_codes", align_bytes=64)
+                plane = w_codes_pool.tile([P, BLK], U8, name="w_plane", align_bytes=64)
+                nc.vector.quantize_mx(
+                    out=codes[:].bitcast(FP8X4), scales=plane[:], in_=grouped[:].rearrange("p n t -> p (n t)")
+                )
+                for m in range(M_TILES):
+                    m_cols = slice(m * P, (m + 1) * P)
+                    if k_pass == 0:
+                        lhs, lhs_plane = in_codes[:, 3 + block, m_cols], in_planes[:, 3 + block, m_cols]
+                    else:
+                        lhs, lhs_plane = x_codes[:, k_pass - 1, m_cols], x_planes[:, k_pass - 1, m_cols]
+                    nc.tensor.matmul_mx(
+                        out=acc[block][m][:],
+                        lhsT=lhs.bitcast(FP8X4),
+                        lhsT_scale=lhs_plane,
+                        rhs=codes[:].bitcast(FP8X4),
+                        rhs_scale=plane[:],
+                        start=(k_pass == 0),
+                        stop=(k_pass == HID_PASSES - 1),
+                    )
+
+        with tc.tile_pool(name="final", bufs=3) as final:
+            for m in range(M_TILES):
+                mean_var, rstd = norm_scalars(nc, small, [acc[g][m] for g in range(BLOCKS)], neg_half)
+                for g in range(BLOCKS):
+                    n_cols = slice(g * BLK, (g + 1) * BLK)
+                    centred = final.tile([P, BLK], F32, name="centred")
+                    nc.vector.scalar_tensor_tensor(
+                        out=centred[:], in0=acc[g][m][:], scalar=mean_var[:, 0:1], in1=out_gain_bias[:, n_cols],
+                        op0=ALU.subtract, op1=ALU.mult,
+                    )
+                    z = final.tile([P, BLK], F32, name="z")
+                    nc.vector.scalar_tensor_tensor(
+                        out=z[:], in0=centred[:], scalar=rstd[:], in1=out_gain_bias[:, DETER + g * BLK : DETER + (g + 1) * BLK],
+                        op0=ALU.mult, op1=ALU.add,
+                    )
+                    result = final.tile([P, BLK], F32, name="result")
+                    nc.scalar.activation(out=result[:], in_=z[:], func=ACT.Silu)
+                    nc.sync.dma_start(out=out[m * P : (m + 1) * P, n_cols], in_=result[:])

@@ -29,24 +29,16 @@ EPS = 1e-3
 FLOPS = 2 * ROWS * ((1024 + 512 + 1536) * HID + BLOCKS * HID_PASSES * K_PASS * BLK)
 
 
+RAW_BUFS = 4
+N_PAIRS = BLOCKS * HID_PASSES // 2
+MAX_PASSES_A_STEP = 4
+
+
 def regroup(copy, grouped, planes):
     copy(
         out=grouped.rearrange("p (c i) t -> p c t i", i=4),
         in_=planes.rearrange("p t (c i) -> p c t i", i=4),
     )
-
-
-def norm_scalars(nc, small, banks, neg_half):
-    stats = small.tile([P, len(banks), 6], F32, name="stats", tag="stats%d" % len(banks))
-    for j, bank in enumerate(banks):
-        nc.vector.bn_stats(out=stats[:, j, :], in_=bank[:])
-    mean_var = small.tile([P, 2], F32, name="mean_var")
-    nc.vector.bn_aggr(out=mean_var[:], in_=stats[:].rearrange("p a b -> p (a b)"))
-    var_eps = small.tile([P, 1], F32, name="var_eps")
-    nc.vector.tensor_scalar_add(out=var_eps[:], in0=mean_var[:, 1:2], scalar1=EPS)
-    rstd = small.tile([P, 1], F32, name="rstd")
-    nc.gpsimd.tensor_tensor(out=rstd[:], in0=var_eps[:], in1=neg_half[:], op=ALU.pow)
-    return mean_var, rstd
 
 
 def tile_blockrecurrentmodel_pa_k_kernel(
@@ -73,10 +65,11 @@ def tile_blockrecurrentmodel_pa_k_kernel(
 ):
     nc = tc.nc
     with ExitStack() as whole:
+        whole.enter_context(tc.manual_schedule())
         consts = whole.enter_context(tc.tile_pool(name="consts", bufs=1))
-        small = whole.enter_context(tc.tile_pool(name="small", bufs=4))
-        w_raw_pool = whole.enter_context(tc.tile_pool(name="w_raw", bufs=5))
-        w_grouped_pool = whole.enter_context(tc.tile_pool(name="w_grouped", bufs=3))
+        small = whole.enter_context(tc.tile_pool(name="small", bufs=3))
+        w_raw_pool = whole.enter_context(tc.tile_pool(name="w_raw", bufs=RAW_BUFS))
+        w_grouped_pool = whole.enter_context(tc.tile_pool(name="w_grouped", bufs=4))
         w_codes_pool = whole.enter_context(tc.tile_pool(name="w_codes", bufs=12))
         psum_bank = whole.enter_context(tc.psum_pool(name="psum_bank", bufs=6))
         psum_tr = whole.enter_context(tc.psum_pool(name="psum_tr", bufs=2))
@@ -96,89 +89,123 @@ def tile_blockrecurrentmodel_pa_k_kernel(
         x_planes = consts.tile([P, 15, ROWS], U8, name="x_planes", align_bytes=64)
         gain_bias = consts.tile([P, PACK, P], F32, name="gain_bias")
         out_gain_bias = consts.tile([P, 2 * DETER], BF16, name="out_gain_bias")
+        out_stats = [consts.tile([P, BLOCKS, 6], F32, name="out_stats%d" % m) for m in range(M_TILES)]
 
-        def load_w_hid_pair(pair):
-            block = pair % BLOCKS
-            first_row = (pair // BLOCKS) * 2 * K_PASS
+        def norm_scalars(stats):
+            mean_var = small.tile([P, 2], F32, name="mean_var")
+            nc.vector.bn_aggr(out=mean_var[:], in_=stats[:].rearrange("p a b -> p (a b)"))
+            var_eps = small.tile([P, 1], F32, name="var_eps")
+            nc.vector.tensor_scalar_add(out=var_eps[:], in0=mean_var[:, 1:2], scalar1=EPS)
+            rstd = small.tile([P, 1], F32, name="rstd")
+            nc.gpsimd.tensor_tensor(out=rstd[:], in0=var_eps[:], in1=neg_half[:], op=ALU.pow)
+            return mean_var, rstd
+
+        w_raw = []
+
+        def load_w_pair(pair):
+            first_row = (pair % (HID_PASSES // 2)) * 2 * K_PASS
             raw = w_raw_pool.tile([P, 2, PACK, BLK], BF16, name="w_raw")
             nc.sync.dma_start(
                 out=raw[:],
-                in_=W_hid[block, first_row : first_row + 2 * K_PASS, :].rearrange(
+                in_=W_hid[pair // (HID_PASSES // 2), first_row : first_row + 2 * K_PASS, :].rearrange(
                     "(c p t) n -> p c t n", c=2, t=PACK
                 ),
             )
-            return raw
+            w_raw.append(raw)
 
-        w_raw = []
+        def w_step(pair, waiting, ready):
+            regrouped = []
+            for c in range(2):
+                grouped = w_grouped_pool.tile([P, BLK, PACK], BF16, name="w_grouped", align_bytes=64)
+                regroup(nc.vector.tensor_copy if c == 0 else nc.scalar.copy, grouped[:], w_raw[pair][:, c, :, :])
+                regrouped.append((grouped, pair // (HID_PASSES // 2), (pair % (HID_PASSES // 2)) * 2 + c))
+            if pair + RAW_BUFS < N_PAIRS:
+                load_w_pair(pair + RAW_BUFS)
+            quantise_w(waiting, ready)
+            return regrouped
+
+        def quantise_w(waiting, ready):
+            for grouped, block, k_pass in waiting:
+                codes = w_codes_pool.tile([P, BLK], U32, name="w_codes", align_bytes=64)
+                plane = w_codes_pool.tile([P, BLK], U8, name="w_plane", align_bytes=64)
+                nc.vector.quantize_mx(
+                    out=codes[:].bitcast(FP8X4), scales=plane[:], in_=grouped[:].rearrange("p n t -> p (n t)")
+                )
+                ready.append((codes, plane, block, k_pass))
+
+        waiting = []
+        ready = []
 
         with ExitStack() as stage1:
             setup = stage1.enter_context(tc.tile_pool(name="setup", bufs=1))
             in_grouped_pool = stage1.enter_context(tc.tile_pool(name="in_grouped", bufs=2))
-            w1_pool = stage1.enter_context(tc.tile_pool(name="w1", bufs=4))
-            u_pool = stage1.enter_context(tc.tile_pool(name="u", bufs=16))
-            xt_pool = stage1.enter_context(tc.tile_pool(name="xt", bufs=2))
+            w1_pool = stage1.enter_context(tc.tile_pool(name="w1", bufs=5))
+            u_pool = stage1.enter_context(tc.tile_pool(name="u", bufs=12))
+            xt_pool = stage1.enter_context(tc.tile_pool(name="xt", bufs=3))
 
-            planes_sa = setup.tile([P, HID], U8, name="planes_sa", align_bytes=64)
+            planes_a = setup.tile([P, HID], U8, name="planes_a", align_bytes=64)
+            planes_s = setup.tile([P, HID], U8, name="planes_s", align_bytes=64)
             planes_d = setup.tile([P, HID], U8, name="planes_d", align_bytes=64)
             vec_rows = setup.tile([P, K_PASS], BF16, name="vec_rows")
             out_vec_row = setup.tile([P, 2 * DETER], BF16, name="out_vec_row")
-            nc.vector.memset(planes_sa[:].bitcast(I32), 0)
+            nc.vector.memset(planes_a[:].bitcast(I32), 0)
+            nc.vector.memset(out_vec_row[:], 0.0)
+            nc.vector.memset(planes_s[:].bitcast(I32), 0)
             nc.vector.memset(planes_d[:].bitcast(I32), 0)
             nc.vector.memset(vec_rows[:], 0.0)
-            nc.vector.memset(out_vec_row[:], 0.0)
 
-            streams = [
-                dict(x=a, k=512, words=W_a_words, first_group=2, planes=planes_sa, plane_row=8,
-                     gain_row=10, bias_row=15, first_pass=5),
-                dict(x=s, k=1024, words=W_s_words, first_group=0, planes=planes_sa, plane_row=0,
-                     gain_row=0, bias_row=5, first_pass=0),
-                dict(x=d, k=1536, words=W_d_words, first_group=3, planes=planes_d, plane_row=0,
-                     gain_row=20, bias_row=25, first_pass=10),
-            ]
+            stream_a = dict(x=a, k=512, words=W_a_words, first_group=2, planes=planes_a,
+                            gain_row=10, bias_row=15, first_pass=5, w=[])
+            stream_s = dict(x=s, k=1024, words=W_s_words, first_group=0, planes=planes_s,
+                            gain_row=0, bias_row=5, first_pass=0, w=[])
+            stream_d = dict(x=d, k=1536, words=W_d_words, first_group=3, planes=planes_d,
+                            gain_row=20, bias_row=25, first_pass=10, w=[])
+            streams = [stream_a, stream_s, stream_d]
 
-            for st in streams:
+            def load_input(st):
                 x_sb = setup.tile([P, M_TILES, st["k"]], BF16, name="x_sb%d" % st["k"])
                 nc.sync.dma_start(
-                    out=x_sb[:],
-                    in_=st["x"].flatten_outer_dims().rearrange("(m p) k -> p m k", p=P),
+                    out=x_sb[:], in_=st["x"].flatten_outer_dims().rearrange("(m p) k -> p m k", p=P)
                 )
                 st["x_sb"] = x_sb
-            for quad in range(4):
-                rows = slice(4 * quad, 4 * quad + 4)
-                nc.sync.dma_start(
-                    out=planes_sa[32 * quad + 8 : 32 * quad + 12, :].bitcast(I32),
-                    in_=W_a_scales[0, rows, :].bitcast(I32),
-                )
-                nc.sync.dma_start(
-                    out=planes_sa[32 * quad : 32 * quad + 8, :].bitcast(I32),
-                    in_=W_s_scales[:, rows, :].bitcast(I32),
-                )
-                nc.sync.dma_start(
-                    out=planes_d[32 * quad : 32 * quad + 12, :].bitcast(I32),
-                    in_=W_d_scales[:, rows, :].bitcast(I32),
-                )
-            for i, st in enumerate(streams):
-                st["w"] = []
-                for g in range(st["k"] // K_PASS):
-                    w = w1_pool.tile([P, HID], U32, name="w1", align_bytes=64)
-                    nc.sync.dma_start(
-                        out=w[:].bitcast(I32),
-                        in_=st["words"][g].rearrange("p n t -> p (n t)").bitcast(I32),
-                    )
-                    st["w"].append(w)
-                if i == 0:
-                    for v, vec in enumerate([ln_s_g, ln_s_b, ln_a_g, ln_a_b, ln_d_g, ln_d_b]):
-                        nc.sync.dma_start(
-                            out=vec_rows[HID_BANKS * v : HID_BANKS * (v + 1), :],
-                            in_=vec.rearrange("(c k) -> c k", k=K_PASS),
-                        )
-                if i < 2:
-                    w_raw.append(load_w_hid_pair(len(w_raw)))
-                    w_raw.append(load_w_hid_pair(len(w_raw)))
-            nc.sync.dma_start(out=out_vec_row[0:1, 0:DETER], in_=ln_h_g.rearrange("(o k) -> o k", o=1))
-            nc.sync.dma_start(out=out_vec_row[0:1, DETER:], in_=ln_h_b.rearrange("(o k) -> o k", o=1))
 
-            for st in streams:
+            def load_words(st, groups, pieces):
+                for g in groups:
+                    w = w1_pool.tile([P, HID], U32, name="w1", align_bytes=64)
+                    words = st["words"][g].rearrange("p n t -> p (n t)").bitcast(I32)
+                    for n_cols in [slice(i * HID // pieces, (i + 1) * HID // pieces) for i in range(pieces)]:
+                        nc.sync.dma_start(out=w[:, n_cols].bitcast(I32), in_=words[:, n_cols])
+                    st["w"].append(w)
+
+            def load_scale_rows(planes, scales):
+                n_rows = 4 * scales.shape[0]
+                for quad in range(4):
+                    nc.sync.dma_start(
+                        out=planes[32 * quad : 32 * quad + n_rows, :].bitcast(I32),
+                        in_=scales[:, 4 * quad : 4 * quad + 4, :].bitcast(I32),
+                    )
+
+            load_input(stream_a)
+            load_scale_rows(planes_a, W_a_scales)
+            load_words(stream_a, [0], HID_BANKS)
+            load_input(stream_s)
+            load_input(stream_d)
+            load_w_pair(0)
+            load_scale_rows(planes_s, W_s_scales)
+            load_words(stream_s, [0, 1], 1)
+            load_w_pair(1)
+            load_scale_rows(planes_d, W_d_scales)
+            load_w_pair(2)
+            load_words(stream_d, [0, 1], 1)
+            load_w_pair(3)
+            nc.gpsimd.dma_start(out=out_vec_row[0:1, 0:DETER], in_=ln_h_g.rearrange("(o k) -> o k", o=1))
+            nc.gpsimd.dma_start(out=out_vec_row[0:1, DETER:], in_=ln_h_b.rearrange("(o k) -> o k", o=1))
+            for v, vec in enumerate([ln_s_g, ln_s_b, ln_a_g, ln_a_b, ln_d_g, ln_d_b]):
+                nc.gpsimd.dma_start(
+                    out=vec_rows[HID_BANKS * v : HID_BANKS * (v + 1), :], in_=vec.rearrange("(c k) -> c k", k=K_PASS)
+                )
+
+            def quantise_input(st):
                 for g in range(st["k"] // K_PASS):
                     group = st["first_group"] + g
                     xt = psum_tr.tile([P, 2, ROWS], F32, name="xt_ps", tag="tr")
@@ -196,134 +223,181 @@ def tile_blockrecurrentmodel_pa_k_kernel(
                         in_=xt[:].rearrange("p h r -> p r h"),
                     )
                     nc.vector.quantize_mx(
-                        out=in_codes[:, group, :].bitcast(FP8X4),
-                        scales=in_planes[:, group, :],
-                        in_=grouped[:],
+                        out=in_codes[:, group, :].bitcast(FP8X4), scales=in_planes[:, group, :], in_=grouped[:]
                     )
 
-            vec_sorted = setup.tile([P, PACK, P], F32, name="vec_sorted")
-            nc.vector.tensor_copy(out=vec_sorted[:], in_=vec_rows[:].rearrange("r (q t) -> r t q", t=PACK))
-            gb_ps = psum_tr.tile([P, PACK, P], F32, name="gb_ps", tag="tr")
-            for t in range(PACK):
-                nc.tensor.transpose(gb_ps[:, t, :], vec_sorted[:, t, :], ident[:])
-            nc.vector.tensor_copy(out=gain_bias[:], in_=gb_ps[:])
+            def sort_gains():
+                vec_sorted = setup.tile([P, PACK, P], F32, name="vec_sorted")
+                nc.vector.tensor_copy(out=vec_sorted[:], in_=vec_rows[:].rearrange("r (q t) -> r t q", t=PACK))
+                gb_ps = psum_tr.tile([P, PACK, P], F32, name="gb_ps", tag="tr")
+                for t in range(PACK):
+                    nc.tensor.transpose(gb_ps[:, t, :], vec_sorted[:, t, :], ident[:])
+                nc.vector.tensor_copy(out=gain_bias[:], in_=gb_ps[:])
 
-            for st in streams:
+            def spread_out_gains():
+                for j in range(2 * DETER // BANK):
+                    n_cols = slice(j * BANK, (j + 1) * BANK)
+                    spread = psum_tr.tile([P, BANK], F32, name="spread", tag="tr")
+                    nc.tensor.matmul(out=spread[:], lhsT=ones[:], rhs=out_vec_row[:, n_cols], start=True, stop=True)
+                    nc.scalar.copy(out=out_gain_bias[:, n_cols], in_=spread[:])
+
+            def embed(st, m):
                 groups = st["k"] // K_PASS
-                u = []
-                for m in range(M_TILES):
-                    m_cols = slice(m * P, (m + 1) * P)
-                    h = []
-                    for j in range(HID_BANKS):
-                        n_cols = slice(j * BANK, (j + 1) * BANK)
-                        bank = psum_bank.tile([P, BANK], F32, name="h", tag="bank")
-                        for g in range(groups):
-                            group = st["first_group"] + g
-                            nc.tensor.matmul_mx(
-                                out=bank[:],
-                                lhsT=in_codes[:, group, m_cols].bitcast(FP8X4),
-                                lhsT_scale=in_planes[:, group, m_cols],
-                                rhs=st["w"][g][:, n_cols].bitcast(FP8X4),
-                                rhs_scale=st["planes"][st["plane_row"] + 4 * g : P, n_cols],
-                                start=(g == 0),
-                                stop=(g == groups - 1),
-                            )
-                        h.append(bank)
-                    mean_var, rstd = norm_scalars(nc, small, h, neg_half)
-                    neg_mean = small.tile([P, 1], F32, name="neg_mean")
-                    nc.vector.tensor_scalar_mul(out=neg_mean[:], in0=mean_var[:, 0:1], scalar1=-1.0)
-                    shift = small.tile([P, 1], F32, name="shift")
-                    nc.gpsimd.tensor_tensor(out=shift[:], in0=neg_mean[:], in1=rstd[:], op=ALU.mult)
-                    u_m = []
-                    for j in range(HID_BANKS):
-                        u_bank = u_pool.tile([P, PACK, P], F32, name="u")
-                        nc.scalar.activation(
-                            out=u_bank[:],
-                            in_=h[j][:].rearrange("p (q t) -> p t q", t=PACK),
-                            func=ACT.Identity,
-                            scale=rstd[:],
-                            bias=shift[:],
-                        )
-                        u_m.append(u_bank)
-                    u.append(u_m)
-
+                m_cols = slice(m * P, (m + 1) * P)
+                h = []
+                stats = small.tile([P, HID_BANKS, 6], F32, name="stats")
                 for j in range(HID_BANKS):
-                    x_t = xt_pool.tile([P, PACK, ROWS], BF16, name="x_t")
-                    for half in range(2):
-                        z_ps = psum_tr.tile([P, 2, ROWS], F32, name="z_ps", tag="tr")
-                        for i in range(2):
-                            for m in range(M_TILES):
-                                nc.tensor.transpose(
-                                    z_ps[:, i, m * P : (m + 1) * P], u[m][j][:, 2 * half + i, :], ident[:]
-                                )
-                        for i in range(2):
-                            t = 2 * half + i
-                            nc.scalar.activation(
-                                out=x_t[:, t, :],
-                                in_=z_ps[:, i, :],
-                                func=ACT.Silu,
-                                scale=gain_bias[:, t, st["gain_row"] + j : st["gain_row"] + j + 1],
-                                bias=gain_bias[:, t, st["bias_row"] + j : st["bias_row"] + j + 1],
-                            )
-                    x_grouped = xt_pool.tile([P, ROWS, PACK], BF16, name="x_grouped", align_bytes=64)
-                    regroup(nc.vector.tensor_copy, x_grouped[:], x_t[:])
+                    n_cols = slice(j * BANK, (j + 1) * BANK)
+                    bank = psum_bank.tile([P, BANK], F32, name="h", tag="bank")
+                    for g in range(groups):
+                        group = st["first_group"] + g
+                        nc.tensor.matmul_mx(
+                            out=bank[:],
+                            lhsT=in_codes[:, group, m_cols].bitcast(FP8X4),
+                            lhsT_scale=in_planes[:, group, m_cols],
+                            rhs=st["w"][g][:, n_cols].bitcast(FP8X4),
+                            rhs_scale=st["planes"][4 * g : P, n_cols],
+                            start=(g == 0),
+                            stop=(g == groups - 1),
+                        )
+                    nc.vector.bn_stats(out=stats[:, j, :], in_=bank[:])
+                    h.append(bank)
+                mean_var, rstd = norm_scalars(stats)
+                neg_mean = small.tile([P, 1], F32, name="neg_mean")
+                nc.vector.tensor_scalar_mul(out=neg_mean[:], in0=mean_var[:, 0:1], scalar1=-1.0)
+                shift = small.tile([P, 1], F32, name="shift")
+                nc.gpsimd.tensor_tensor(out=shift[:], in0=neg_mean[:], in1=rstd[:], op=ALU.mult)
+                return h, rstd, shift
+
+            def normalise(h, rstd, shift):
+                u_m = []
+                for j in range(HID_BANKS):
+                    u_bank = u_pool.tile([P, PACK, P], F32, name="u")
+                    nc.scalar.activation(
+                        out=u_bank[:],
+                        in_=h[j][:].rearrange("p (q t) -> p t q", t=PACK),
+                        func=ACT.Identity,
+                        scale=rstd[:],
+                        bias=shift[:],
+                    )
+                    u_m.append(u_bank)
+                return u_m
+
+            def x_pass(st, u, j):
+                x_t = xt_pool.tile([P, PACK, ROWS], BF16, name="x_t")
+                for half in range(2):
+                    z_ps = psum_tr.tile([P, 2, ROWS], F32, name="z_ps", tag="tr")
+                    for i in range(2):
+                        for m in range(M_TILES):
+                            nc.tensor.transpose(z_ps[:, i, m * P : (m + 1) * P], u[m][j][:, 2 * half + i, :], ident[:])
+                    for i in range(2):
+                        t = 2 * half + i
+                        nc.scalar.activation(
+                            out=x_t[:, t, :],
+                            in_=z_ps[:, i, :],
+                            func=ACT.Silu,
+                            scale=gain_bias[:, t, st["gain_row"] + j : st["gain_row"] + j + 1],
+                            bias=gain_bias[:, t, st["bias_row"] + j : st["bias_row"] + j + 1],
+                        )
+                x_grouped = xt_pool.tile([P, ROWS, PACK], BF16, name="x_grouped", align_bytes=64)
+                regroup(nc.vector.tensor_copy, x_grouped[:], x_t[:])
+                return st["first_pass"] + j, x_grouped
+
+            def quantise_x(passes):
+                for k_pass, x_grouped in passes:
                     nc.vector.quantize_mx(
-                        out=x_codes[:, st["first_pass"] + j, :].bitcast(FP8X4),
-                        scales=x_planes[:, st["first_pass"] + j, :],
+                        out=x_codes[:, k_pass, :].bitcast(FP8X4),
+                        scales=x_planes[:, k_pass, :],
                         in_=x_grouped[:].rearrange("p n t -> p (n t)"),
                     )
 
-            for j in range(2 * DETER // BANK):
-                n_cols = slice(j * BANK, (j + 1) * BANK)
-                spread = psum_tr.tile([P, BANK], F32, name="spread", tag="tr")
-                nc.tensor.matmul(out=spread[:], lhsT=ones[:], rhs=out_vec_row[:, n_cols], start=True, stop=True)
-                nc.scalar.copy(out=out_gain_bias[:, n_cols], in_=spread[:])
-
-        acc = [[psum_bank.tile([P, BANK], F32, name="acc", tag="bank") for m in range(M_TILES)] for g in range(BLOCKS)]
-        for pair in range(BLOCKS * HID_PASSES // 2):
-            if pair >= len(w_raw):
-                w_raw.append(load_w_hid_pair(pair))
-            block = pair % BLOCKS
-            for c in range(2):
-                k_pass = (pair // BLOCKS) * 2 + c
-                grouped = w_grouped_pool.tile([P, BLK, PACK], BF16, name="w_grouped", align_bytes=64)
-                regroup(nc.vector.tensor_copy if c == 0 else nc.scalar.copy, grouped[:], w_raw[pair][:, c, :, :])
-                codes = w_codes_pool.tile([P, BLK], U32, name="w_codes", align_bytes=64)
-                plane = w_codes_pool.tile([P, BLK], U8, name="w_plane", align_bytes=64)
-                nc.vector.quantize_mx(
-                    out=codes[:].bitcast(FP8X4), scales=plane[:], in_=grouped[:].rearrange("p n t -> p (n t)")
-                )
+            quantise_input(stream_a)
+            before = None
+            for i, st in enumerate(streams):
+                u = []
                 for m in range(M_TILES):
-                    m_cols = slice(m * P, (m + 1) * P)
-                    if k_pass == 0:
-                        lhs, lhs_plane = in_codes[:, 3 + block, m_cols], in_planes[:, 3 + block, m_cols]
-                    else:
-                        lhs, lhs_plane = x_codes[:, k_pass - 1, m_cols], x_planes[:, k_pass - 1, m_cols]
-                    nc.tensor.matmul_mx(
-                        out=acc[block][m][:],
-                        lhsT=lhs.bitcast(FP8X4),
-                        lhsT_scale=lhs_plane,
-                        rhs=codes[:].bitcast(FP8X4),
-                        rhs_scale=plane[:],
-                        start=(k_pass == 0),
-                        stop=(k_pass == HID_PASSES - 1),
-                    )
+                    unit = M_TILES * i + m
+                    h, rstd, shift = embed(st, m)
+                    if unit == 0:
+                        spread_out_gains()
+                        quantise_input(stream_s)
+                    if unit == 1:
+                        load_words(stream_d, [2], 1)
+                        quantise_input(stream_d)
+                    if unit == 2:
+                        sort_gains()
+                    if unit > 0:
+                        waiting = w_step(unit - 1, waiting, ready)
+                    if before is not None:
+                        quantise_x([x_pass(before[0], before[1], j) for j in ((0, 1, 2) if m == 0 else (3, 4))])
+                    u.append(normalise(h, rstd, shift))
+                before = (st, u)
 
-        with tc.tile_pool(name="final", bufs=3) as final:
+            acc = [
+                [psum_bank.tile([P, BANK], F32, name="acc", tag="bank") for m in range(M_TILES)] for g in range(BLOCKS)
+            ]
+
+            def multiply_ready(chunks, x_done):
+                left = []
+                for i, (codes, plane, block, k_pass) in enumerate(chunks):
+                    if k_pass > x_done or i >= MAX_PASSES_A_STEP:
+                        left.append((codes, plane, block, k_pass))
+                    else:
+                        for m in range(M_TILES):
+                            m_cols = slice(m * P, (m + 1) * P)
+                            if k_pass == 0:
+                                lhs, lhs_plane = in_codes[:, 3 + block, m_cols], in_planes[:, 3 + block, m_cols]
+                            else:
+                                lhs, lhs_plane = x_codes[:, k_pass - 1, m_cols], x_planes[:, k_pass - 1, m_cols]
+                            nc.tensor.matmul_mx(
+                                out=acc[block][m][:],
+                                lhsT=lhs.bitcast(FP8X4),
+                                lhsT_scale=lhs_plane,
+                                rhs=codes[:].bitcast(FP8X4),
+                                rhs_scale=plane[:],
+                                start=(k_pass == 0),
+                                stop=(k_pass == HID_PASSES - 1),
+                            )
+                        if k_pass == HID_PASSES - 1:
+                            for m in range(M_TILES):
+                                nc.vector.bn_stats(out=out_stats[m][:, block, :], in_=acc[block][m][:])
+                return left
+
+            next_pair = M_TILES * len(streams) - 1
+            x_waiting = []
+            for j in range(HID_BANKS):
+                waiting = w_step(next_pair + j, waiting, ready)
+                quantise_x(x_waiting)
+                x_waiting = [x_pass(before[0], before[1], j)]
+                ready = multiply_ready(ready, 2 * HID_BANKS + j)
+            quantise_x(x_waiting)
+            next_pair = next_pair + HID_BANKS
+
+        for pair in range(next_pair, N_PAIRS):
+            waiting = w_step(pair, waiting, ready)
+            ready = multiply_ready(ready, HID_PASSES)
+        quantise_w(waiting, ready)
+        while ready:
+            ready = multiply_ready(ready, HID_PASSES)
+
+        with tc.tile_pool(name="final", bufs=6) as final:
+            scalars = [norm_scalars(out_stats[m]) for m in range(M_TILES)]
             for m in range(M_TILES):
-                mean_var, rstd = norm_scalars(nc, small, [acc[g][m] for g in range(BLOCKS)], neg_half)
+                mean_var, rstd = scalars[m]
+                centred = []
                 for g in range(BLOCKS):
-                    n_cols = slice(g * BLK, (g + 1) * BLK)
-                    centred = final.tile([P, BLK], F32, name="centred")
+                    c_tile = final.tile([P, BLK], F32, name="centred")
                     nc.vector.scalar_tensor_tensor(
-                        out=centred[:], in0=acc[g][m][:], scalar=mean_var[:, 0:1], in1=out_gain_bias[:, n_cols],
-                        op0=ALU.subtract, op1=ALU.mult,
+                        out=c_tile[:], in0=acc[g][m][:], scalar=mean_var[:, 0:1],
+                        in1=out_gain_bias[:, g * BLK : (g + 1) * BLK], op0=ALU.subtract, op1=ALU.mult,
                     )
+                    centred.append(c_tile)
+                for g in range(BLOCKS):
                     z = final.tile([P, BLK], F32, name="z")
                     nc.vector.scalar_tensor_tensor(
-                        out=z[:], in0=centred[:], scalar=rstd[:], in1=out_gain_bias[:, DETER + g * BLK : DETER + (g + 1) * BLK],
-                        op0=ALU.mult, op1=ALU.add,
+                        out=z[:], in0=centred[g][:], scalar=rstd[:],
+                        in1=out_gain_bias[:, DETER + g * BLK : DETER + (g + 1) * BLK], op0=ALU.mult, op1=ALU.add,
                     )
                     result = final.tile([P, BLK], F32, name="result")
                     nc.scalar.activation(out=result[:], in_=z[:], func=ACT.Silu)
-                    nc.sync.dma_start(out=out[m * P : (m + 1) * P, n_cols], in_=result[:])
+                    nc.sync.dma_start(out=out[m * P : (m + 1) * P, g * BLK : (g + 1) * BLK], in_=result[:])

@@ -263,10 +263,10 @@ def tile_blockrecurrentmodel_pa_k_kernel(
                     nc.vector.bn_stats(out=stats[:, j, :], in_=bank[:])
                     h.append(bank)
                 mean_var, rstd = norm_scalars(stats)
-                neg_mean = small.tile([P, 1], F32, name="neg_mean")
-                nc.vector.tensor_scalar_mul(out=neg_mean[:], in0=mean_var[:, 0:1], scalar1=-1.0)
                 shift = small.tile([P, 1], F32, name="shift")
-                nc.gpsimd.tensor_tensor(out=shift[:], in0=neg_mean[:], in1=rstd[:], op=ALU.mult)
+                nc.vector.scalar_tensor_tensor(
+                    out=shift[:], in0=mean_var[:, 0:1], scalar=-1.0, in1=rstd[:], op0=ALU.mult, op1=ALU.mult
+                )
                 return h, rstd, shift
 
             def normalise(h, rstd, shift):

@@ -23,15 +23,19 @@ HID_BANKS = HID // BANK
 DETER = 1536
 BLOCKS = 3
 BLK = DETER // BLOCKS
-HID_PASSES = 1 + 3 * HID // K_PASS
+X_PASSES = 3 * HID_BANKS
+HID_PASSES = 1 + X_PASSES
+N_PAIRS = BLOCKS * HID_PASSES // 2
 EPS = 1e-3
 
 FLOPS = 2 * ROWS * ((1024 + 512 + 1536) * HID + BLOCKS * HID_PASSES * K_PASS * BLK)
 
-
+X_LAG = 8
+W_START = 5
+N_SLOTS = W_START + N_PAIRS
 RAW_BUFS = 4
-N_PAIRS = BLOCKS * HID_PASSES // 2
-MAX_PASSES_A_STEP = 4
+W1_BUFS = 5
+MAX_PASSES_A_SLOT = 4
 
 
 def regroup(copy, grouped, planes):
@@ -67,11 +71,12 @@ def tile_blockrecurrentmodel_pa_k_kernel(
     with ExitStack() as whole:
         whole.enter_context(tc.manual_schedule())
         consts = whole.enter_context(tc.tile_pool(name="consts", bufs=1))
-        small = whole.enter_context(tc.tile_pool(name="small", bufs=3))
+        small = whole.enter_context(tc.tile_pool(name="small", bufs=4))
         w_raw_pool = whole.enter_context(tc.tile_pool(name="w_raw", bufs=RAW_BUFS))
         w_grouped_pool = whole.enter_context(tc.tile_pool(name="w_grouped", bufs=4))
-        w_codes_pool = whole.enter_context(tc.tile_pool(name="w_codes", bufs=12))
-        psum_bank = whole.enter_context(tc.psum_pool(name="psum_bank", bufs=6))
+        w_codes_pool = whole.enter_context(tc.tile_pool(name="w_codes", bufs=14))
+        psum_acc = whole.enter_context(tc.psum_pool(name="psum_acc", bufs=4))
+        psum_h = whole.enter_context(tc.psum_pool(name="psum_h", bufs=2))
         psum_tr = whole.enter_context(tc.psum_pool(name="psum_tr", bufs=2))
 
         ident = consts.tile([P, P], F32, name="ident")
@@ -85,8 +90,8 @@ def tile_blockrecurrentmodel_pa_k_kernel(
 
         in_codes = consts.tile([P, 6, ROWS], U32, name="in_codes", align_bytes=64)
         in_planes = consts.tile([P, 6, ROWS], U8, name="in_planes", align_bytes=64)
-        x_codes = consts.tile([P, 15, ROWS], U32, name="x_codes", align_bytes=64)
-        x_planes = consts.tile([P, 15, ROWS], U8, name="x_planes", align_bytes=64)
+        x_codes = consts.tile([P, X_PASSES, ROWS], U32, name="x_codes", align_bytes=64)
+        x_planes = consts.tile([P, X_PASSES, ROWS], U8, name="x_planes", align_bytes=64)
         gain_bias = consts.tile([P, PACK, P], F32, name="gain_bias")
         out_gain_bias = consts.tile([P, 2 * DETER], BF16, name="out_gain_bias")
         out_stats = [consts.tile([P, BLOCKS, 6], F32, name="out_stats%d" % m) for m in range(M_TILES)]
@@ -100,47 +105,11 @@ def tile_blockrecurrentmodel_pa_k_kernel(
             nc.gpsimd.tensor_tensor(out=rstd[:], in0=var_eps[:], in1=neg_half[:], op=ALU.pow)
             return mean_var, rstd
 
-        w_raw = []
-
-        def load_w_pair(pair):
-            first_row = (pair % (HID_PASSES // 2)) * 2 * K_PASS
-            raw = w_raw_pool.tile([P, 2, PACK, BLK], BF16, name="w_raw")
-            nc.sync.dma_start(
-                out=raw[:],
-                in_=W_hid[pair // (HID_PASSES // 2), first_row : first_row + 2 * K_PASS, :].rearrange(
-                    "(c p t) n -> p c t n", c=2, t=PACK
-                ),
-            )
-            w_raw.append(raw)
-
-        def w_step(pair, waiting, ready):
-            regrouped = []
-            for c in range(2):
-                grouped = w_grouped_pool.tile([P, BLK, PACK], BF16, name="w_grouped", align_bytes=64)
-                regroup(nc.vector.tensor_copy if c == 0 else nc.scalar.copy, grouped[:], w_raw[pair][:, c, :, :])
-                regrouped.append((grouped, pair // (HID_PASSES // 2), (pair % (HID_PASSES // 2)) * 2 + c))
-            if pair + RAW_BUFS < N_PAIRS:
-                load_w_pair(pair + RAW_BUFS)
-            quantise_w(waiting, ready)
-            return regrouped
-
-        def quantise_w(waiting, ready):
-            for grouped, block, k_pass in waiting:
-                codes = w_codes_pool.tile([P, BLK], U32, name="w_codes", align_bytes=64)
-                plane = w_codes_pool.tile([P, BLK], U8, name="w_plane", align_bytes=64)
-                nc.vector.quantize_mx(
-                    out=codes[:].bitcast(FP8X4), scales=plane[:], in_=grouped[:].rearrange("p n t -> p (n t)")
-                )
-                ready.append((codes, plane, block, k_pass))
-
-        waiting = []
-        ready = []
-
         with ExitStack() as stage1:
             setup = stage1.enter_context(tc.tile_pool(name="setup", bufs=1))
             in_grouped_pool = stage1.enter_context(tc.tile_pool(name="in_grouped", bufs=2))
-            w1_pool = stage1.enter_context(tc.tile_pool(name="w1", bufs=5))
-            u_pool = stage1.enter_context(tc.tile_pool(name="u", bufs=12))
+            w1_pool = stage1.enter_context(tc.tile_pool(name="w1", bufs=W1_BUFS))
+            u_pool = stage1.enter_context(tc.tile_pool(name="u", bufs=18))
             xt_pool = stage1.enter_context(tc.tile_pool(name="xt", bufs=3))
 
             planes_a = setup.tile([P, HID], U8, name="planes_a", align_bytes=64)
@@ -154,28 +123,30 @@ def tile_blockrecurrentmodel_pa_k_kernel(
             nc.vector.memset(planes_d[:].bitcast(I32), 0)
             nc.vector.memset(vec_rows[:], 0.0)
 
-            stream_a = dict(x=a, k=512, words=W_a_words, first_group=2, planes=planes_a,
-                            gain_row=10, bias_row=15, first_pass=5, w=[])
-            stream_s = dict(x=s, k=1024, words=W_s_words, first_group=0, planes=planes_s,
-                            gain_row=0, bias_row=5, first_pass=0, w=[])
-            stream_d = dict(x=d, k=1536, words=W_d_words, first_group=3, planes=planes_d,
-                            gain_row=20, bias_row=25, first_pass=10, w=[])
+            stream_a = dict(x=a, groups=1, words=W_a_words, first_group=2, planes=planes_a,
+                            gain_row=10, bias_row=15, first_pass=5)
+            stream_s = dict(x=s, groups=2, words=W_s_words, first_group=0, planes=planes_s,
+                            gain_row=0, bias_row=5, first_pass=0)
+            stream_d = dict(x=d, groups=3, words=W_d_words, first_group=3, planes=planes_d,
+                            gain_row=20, bias_row=25, first_pass=10)
             streams = [stream_a, stream_s, stream_d]
 
+            pass_order = [(1 + stream_a["first_pass"] + j, 1 + j) for j in range(HID_BANKS)]
+            pass_order.append((0, 0))
+            pass_order.extend([(1 + stream_s["first_pass"] + j, HID_BANKS + 1 + j) for j in range(HID_BANKS)])
+            pass_order.extend([(1 + stream_d["first_pass"] + j, 2 * HID_BANKS + 1 + j) for j in range(HID_BANKS)])
+
+            def pair_place(pair, c):
+                if pair < HID_PASSES:
+                    return pair % 2, 2 * (pair // 2) + c
+                return 2, 2 * (pair - HID_PASSES) + c
+
             def load_input(st):
-                x_sb = setup.tile([P, M_TILES, st["k"]], BF16, name="x_sb%d" % st["k"])
+                x_sb = setup.tile([P, M_TILES, st["groups"] * K_PASS], BF16, name="x_sb%d" % st["groups"])
                 nc.sync.dma_start(
                     out=x_sb[:], in_=st["x"].flatten_outer_dims().rearrange("(m p) k -> p m k", p=P)
                 )
                 st["x_sb"] = x_sb
-
-            def load_words(st, groups, pieces):
-                for g in groups:
-                    w = w1_pool.tile([P, HID], U32, name="w1", align_bytes=64)
-                    words = st["words"][g].rearrange("p n t -> p (n t)").bitcast(I32)
-                    for n_cols in [slice(i * HID // pieces, (i + 1) * HID // pieces) for i in range(pieces)]:
-                        nc.sync.dma_start(out=w[:, n_cols].bitcast(I32), in_=words[:, n_cols])
-                    st["w"].append(w)
 
             def load_scale_rows(planes, scales):
                 n_rows = 4 * scales.shape[0]
@@ -185,19 +156,42 @@ def tile_blockrecurrentmodel_pa_k_kernel(
                         in_=scales[:, 4 * quad : 4 * quad + 4, :].bitcast(I32),
                     )
 
+            w1 = []
+
+            def load_w1(slot):
+                st = streams[slot // HID_BANKS]
+                n_bytes = slice((slot % HID_BANKS) * BANK * PACK, (slot % HID_BANKS + 1) * BANK * PACK)
+                words = w1_pool.tile([P, 3, BANK], U32, name="w1", align_bytes=64)
+                for g in range(st["groups"]):
+                    nc.sync.dma_start(
+                        out=words[:, g, :].bitcast(I32),
+                        in_=st["words"][g].rearrange("p n t -> p (n t)")[:, n_bytes].bitcast(I32),
+                    )
+                w1.append(words)
+
+            w_raw = []
+
+            def load_w_pair(pair):
+                raw = w_raw_pool.tile([P, 2, PACK, BLK], BF16, name="w_raw")
+                for c in range(2):
+                    block, pos = pair_place(pair, c)
+                    first_row = pass_order[pos][0] * K_PASS
+                    nc.sync.dma_start(
+                        out=raw[:, c, :, :],
+                        in_=W_hid[block, first_row : first_row + K_PASS, :].rearrange("(p t) n -> p t n", t=PACK),
+                    )
+                w_raw.append(raw)
+
             load_input(stream_a)
             load_scale_rows(planes_a, W_a_scales)
-            load_words(stream_a, [0], HID_BANKS)
+            for slot in range(W1_BUFS):
+                load_w1(slot)
             load_input(stream_s)
             load_input(stream_d)
-            load_w_pair(0)
+            for pair in range(RAW_BUFS - W_START):
+                load_w_pair(pair)
             load_scale_rows(planes_s, W_s_scales)
-            load_words(stream_s, [0, 1], 1)
-            load_w_pair(1)
             load_scale_rows(planes_d, W_d_scales)
-            load_w_pair(2)
-            load_words(stream_d, [0, 1], 1)
-            load_w_pair(3)
             nc.gpsimd.dma_start(out=out_vec_row[0:1, 0:DETER], in_=ln_h_g.rearrange("(o k) -> o k", o=1))
             nc.gpsimd.dma_start(out=out_vec_row[0:1, DETER:], in_=ln_h_b.rearrange("(o k) -> o k", o=1))
             for v, vec in enumerate([ln_s_g, ln_s_b, ln_a_g, ln_a_b, ln_d_g, ln_d_b]):
@@ -205,26 +199,22 @@ def tile_blockrecurrentmodel_pa_k_kernel(
                     out=vec_rows[HID_BANKS * v : HID_BANKS * (v + 1), :], in_=vec.rearrange("(c k) -> c k", k=K_PASS)
                 )
 
-            def quantise_input(st):
-                for g in range(st["k"] // K_PASS):
-                    group = st["first_group"] + g
-                    xt = psum_tr.tile([P, 2, ROWS], F32, name="xt_ps", tag="tr")
-                    for half in range(2):
-                        for m in range(M_TILES):
-                            words = st["x_sb"][:, m, :].bitcast(F32)
-                            nc.tensor.transpose(
-                                xt[:, half, m * P : (m + 1) * P],
-                                words[:, 256 * g + half : 256 * (g + 1) : 2],
-                                ident[:],
-                            )
-                    grouped = in_grouped_pool.tile([P, ROWS * PACK], BF16, name="in_grouped", align_bytes=64)
-                    nc.scalar.copy(
-                        out=grouped[:].bitcast(F32).rearrange("p (r h) -> p r h", h=2),
-                        in_=xt[:].rearrange("p h r -> p r h"),
-                    )
-                    nc.vector.quantize_mx(
-                        out=in_codes[:, group, :].bitcast(FP8X4), scales=in_planes[:, group, :], in_=grouped[:]
-                    )
+            def quantise_input(st, g):
+                xt = psum_tr.tile([P, 2, ROWS], F32, name="xt_ps", tag="tr")
+                for half in range(2):
+                    for m in range(M_TILES):
+                        words = st["x_sb"][:, m, :].bitcast(F32)
+                        nc.tensor.transpose(
+                            xt[:, half, m * P : (m + 1) * P], words[:, 256 * g + half : 256 * (g + 1) : 2], ident[:]
+                        )
+                grouped = in_grouped_pool.tile([P, ROWS * PACK], BF16, name="in_grouped", align_bytes=64)
+                nc.scalar.copy(
+                    out=grouped[:].bitcast(F32).rearrange("p (r h) -> p r h", h=2), in_=xt[:].rearrange("p h r -> p r h")
+                )
+                group = st["first_group"] + g
+                nc.vector.quantize_mx(
+                    out=in_codes[:, group, :].bitcast(FP8X4), scales=in_planes[:, group, :], in_=grouped[:]
+                )
 
             def sort_gains():
                 vec_sorted = setup.tile([P, PACK, P], F32, name="vec_sorted")
@@ -234,156 +224,200 @@ def tile_blockrecurrentmodel_pa_k_kernel(
                     nc.tensor.transpose(gb_ps[:, t, :], vec_sorted[:, t, :], ident[:])
                 nc.vector.tensor_copy(out=gain_bias[:], in_=gb_ps[:])
 
-            def spread_out_gains():
-                for j in range(2 * DETER // BANK):
-                    n_cols = slice(j * BANK, (j + 1) * BANK)
-                    spread = psum_tr.tile([P, BANK], F32, name="spread", tag="tr")
-                    nc.tensor.matmul(out=spread[:], lhsT=ones[:], rhs=out_vec_row[:, n_cols], start=True, stop=True)
-                    nc.scalar.copy(out=out_gain_bias[:, n_cols], in_=spread[:])
+            def spread_out_gains(piece):
+                n_cols = slice(piece * BANK, (piece + 1) * BANK)
+                spread = psum_tr.tile([P, BANK], F32, name="spread", tag="tr")
+                nc.tensor.matmul(out=spread[:], lhsT=ones[:], rhs=out_vec_row[:, n_cols], start=True, stop=True)
+                nc.scalar.copy(out=out_gain_bias[:, n_cols], in_=spread[:])
 
-            def embed(st, m):
-                groups = st["k"] // K_PASS
-                m_cols = slice(m * P, (m + 1) * P)
-                h = []
-                stats = small.tile([P, HID_BANKS, 6], F32, name="stats")
-                for j in range(HID_BANKS):
-                    n_cols = slice(j * BANK, (j + 1) * BANK)
-                    bank = psum_bank.tile([P, BANK], F32, name="h", tag="bank")
-                    for g in range(groups):
+            def embed(slot):
+                st = streams[slot // HID_BANKS]
+                n_cols = slice((slot % HID_BANKS) * BANK, (slot % HID_BANKS + 1) * BANK)
+                banks = []
+                for m in range(M_TILES):
+                    m_cols = slice(m * P, (m + 1) * P)
+                    bank = psum_h.tile([P, BANK], F32, name="h", tag="h")
+                    for g in range(st["groups"]):
                         group = st["first_group"] + g
                         nc.tensor.matmul_mx(
                             out=bank[:],
                             lhsT=in_codes[:, group, m_cols].bitcast(FP8X4),
                             lhsT_scale=in_planes[:, group, m_cols],
-                            rhs=st["w"][g][:, n_cols].bitcast(FP8X4),
+                            rhs=w1[slot][:, g, :].bitcast(FP8X4),
                             rhs_scale=st["planes"][4 * g : P, n_cols],
                             start=(g == 0),
-                            stop=(g == groups - 1),
+                            stop=(g == st["groups"] - 1),
                         )
-                    nc.vector.bn_stats(out=stats[:, j, :], in_=bank[:])
-                    h.append(bank)
-                mean_var, rstd = norm_scalars(stats)
-                shift = small.tile([P, 1], F32, name="shift")
-                nc.vector.scalar_tensor_tensor(
-                    out=shift[:], in0=mean_var[:, 0:1], scalar=-1.0, in1=rstd[:], op0=ALU.mult, op1=ALU.mult
+                    banks.append(bank)
+                return banks
+
+            def copy_out(banks):
+                tiles = []
+                for bank in banks:
+                    u = u_pool.tile([P, PACK, P], F32, name="u")
+                    nc.scalar.copy(out=u[:], in_=bank[:].rearrange("p (q t) -> p t q", t=PACK))
+                    tiles.append(u)
+                return tiles
+
+            def normalise(tiles, scalars):
+                mean_var, rstd = scalars[0][0], scalars[0][1]
+                nc.vector.tensor_scalar(
+                    out=tiles[0][:], in0=tiles[0][:], scalar1=mean_var[:, 0:1], scalar2=rstd[:],
+                    op0=ALU.subtract, op1=ALU.mult,
                 )
-                return h, rstd, shift
+                nc.scalar.activation(
+                    out=tiles[1][:], in_=tiles[1][:], func=ACT.Identity, scale=scalars[1][1][:], bias=scalars[1][2][:]
+                )
 
-            def normalise(h, rstd, shift):
-                u_m = []
-                for j in range(HID_BANKS):
-                    u_bank = u_pool.tile([P, PACK, P], F32, name="u")
-                    nc.scalar.activation(
-                        out=u_bank[:],
-                        in_=h[j][:].rearrange("p (q t) -> p t q", t=PACK),
-                        func=ACT.Identity,
-                        scale=rstd[:],
-                        bias=shift[:],
-                    )
-                    u_m.append(u_bank)
-                return u_m
-
-            def x_pass(st, u, j):
-                x_t = xt_pool.tile([P, PACK, ROWS], BF16, name="x_t")
+            def transpose_pass(tiles):
+                z = []
                 for half in range(2):
                     z_ps = psum_tr.tile([P, 2, ROWS], F32, name="z_ps", tag="tr")
                     for i in range(2):
                         for m in range(M_TILES):
-                            nc.tensor.transpose(z_ps[:, i, m * P : (m + 1) * P], u[m][j][:, 2 * half + i, :], ident[:])
-                    for i in range(2):
-                        t = 2 * half + i
-                        nc.scalar.activation(
-                            out=x_t[:, t, :],
-                            in_=z_ps[:, i, :],
-                            func=ACT.Silu,
-                            scale=gain_bias[:, t, st["gain_row"] + j : st["gain_row"] + j + 1],
-                            bias=gain_bias[:, t, st["bias_row"] + j : st["bias_row"] + j + 1],
-                        )
-                x_grouped = xt_pool.tile([P, ROWS, PACK], BF16, name="x_grouped", align_bytes=64)
-                regroup(nc.vector.tensor_copy, x_grouped[:], x_t[:])
-                return st["first_pass"] + j, x_grouped
+                            nc.tensor.transpose(z_ps[:, i, m * P : (m + 1) * P], tiles[m][:, 2 * half + i, :], ident[:])
+                    z.append(z_ps)
+                return z
 
-            def quantise_x(passes):
-                for k_pass, x_grouped in passes:
-                    nc.vector.quantize_mx(
-                        out=x_codes[:, k_pass, :].bitcast(FP8X4),
-                        scales=x_planes[:, k_pass, :],
-                        in_=x_grouped[:].rearrange("p n t -> p (n t)"),
+            def silu_pass(xp, z):
+                st, j = streams[xp // HID_BANKS], xp % HID_BANKS
+                x_t = xt_pool.tile([P, PACK, ROWS], BF16, name="x_t")
+                for t in range(PACK):
+                    nc.scalar.activation(
+                        out=x_t[:, t, :],
+                        in_=z[t // 2][:, t % 2, :],
+                        func=ACT.Silu,
+                        scale=gain_bias[:, t, st["gain_row"] + j : st["gain_row"] + j + 1],
+                        bias=gain_bias[:, t, st["bias_row"] + j : st["bias_row"] + j + 1],
                     )
+                return x_t
 
-            quantise_input(stream_a)
-            before = None
-            for i, st in enumerate(streams):
-                u = []
-                for m in range(M_TILES):
-                    unit = M_TILES * i + m
-                    h, rstd, shift = embed(st, m)
-                    if unit == 0:
-                        spread_out_gains()
-                        quantise_input(stream_s)
-                    if unit == 1:
-                        load_words(stream_d, [2], 1)
-                        quantise_input(stream_d)
-                    if unit == 2:
-                        sort_gains()
-                    if unit > 0:
-                        waiting = w_step(unit - 1, waiting, ready)
-                    if before is not None:
-                        quantise_x([x_pass(before[0], before[1], j) for j in ((0, 1, 2) if m == 0 else (3, 4))])
-                    u.append(normalise(h, rstd, shift))
-                before = (st, u)
+            def quantise_x(xp, x_grouped):
+                k_pass = streams[xp // HID_BANKS]["first_pass"] + xp % HID_BANKS
+                nc.vector.quantize_mx(
+                    out=x_codes[:, k_pass, :].bitcast(FP8X4),
+                    scales=x_planes[:, k_pass, :],
+                    in_=x_grouped[:].rearrange("p n t -> p (n t)"),
+                )
 
-            acc = [
-                [psum_bank.tile([P, BANK], F32, name="acc", tag="bank") for m in range(M_TILES)] for g in range(BLOCKS)
-            ]
+            def quantise_w(waiting, ready):
+                for grouped, block, pos in waiting:
+                    codes = w_codes_pool.tile([P, BLK], U32, name="w_codes", align_bytes=64)
+                    plane = w_codes_pool.tile([P, BLK], U8, name="w_plane", align_bytes=64)
+                    nc.vector.quantize_mx(
+                        out=codes[:].bitcast(FP8X4), scales=plane[:], in_=grouped[:].rearrange("p n t -> p (n t)")
+                    )
+                    ready.append((codes, plane, block, pos))
+
+            acc = [[psum_acc.tile([P, BANK], F32, name="acc") for m in range(M_TILES)] for block in range(2)]
 
             def multiply_ready(chunks, x_done):
-                left = []
-                for i, (codes, plane, block, k_pass) in enumerate(chunks):
-                    if k_pass > x_done or i >= MAX_PASSES_A_STEP:
-                        left.append((codes, plane, block, k_pass))
-                    else:
+                n = 0
+                while n < min(len(chunks), MAX_PASSES_A_SLOT) and pass_order[chunks[n][3]][1] <= x_done:
+                    codes, plane, block, pos = chunks[n]
+                    k_pass = pass_order[pos][0]
+                    if block == len(acc):
+                        acc.append([psum_h.tile([P, BANK], F32, name="acc_last", tag="h") for m in range(M_TILES)])
+                    for m in range(M_TILES):
+                        m_cols = slice(m * P, (m + 1) * P)
+                        if k_pass == 0:
+                            lhs, lhs_plane = in_codes[:, 3 + block, m_cols], in_planes[:, 3 + block, m_cols]
+                        else:
+                            lhs, lhs_plane = x_codes[:, k_pass - 1, m_cols], x_planes[:, k_pass - 1, m_cols]
+                        nc.tensor.matmul_mx(
+                            out=acc[block][m][:],
+                            lhsT=lhs.bitcast(FP8X4),
+                            lhsT_scale=lhs_plane,
+                            rhs=codes[:].bitcast(FP8X4),
+                            rhs_scale=plane[:],
+                            start=(pos == 0),
+                            stop=(pos == HID_PASSES - 1),
+                        )
+                    if pos == HID_PASSES - 1:
                         for m in range(M_TILES):
-                            m_cols = slice(m * P, (m + 1) * P)
-                            if k_pass == 0:
-                                lhs, lhs_plane = in_codes[:, 3 + block, m_cols], in_planes[:, 3 + block, m_cols]
-                            else:
-                                lhs, lhs_plane = x_codes[:, k_pass - 1, m_cols], x_planes[:, k_pass - 1, m_cols]
-                            nc.tensor.matmul_mx(
-                                out=acc[block][m][:],
-                                lhsT=lhs.bitcast(FP8X4),
-                                lhsT_scale=lhs_plane,
-                                rhs=codes[:].bitcast(FP8X4),
-                                rhs_scale=plane[:],
-                                start=(k_pass == 0),
-                                stop=(k_pass == HID_PASSES - 1),
-                            )
-                        if k_pass == HID_PASSES - 1:
-                            for m in range(M_TILES):
-                                nc.vector.bn_stats(out=out_stats[m][:, block, :], in_=acc[block][m][:])
-                return left
+                            nc.vector.bn_stats(out=out_stats[m][:, block, :], in_=acc[block][m][:])
+                    n = n + 1
+                return chunks[n:]
 
-            next_pair = M_TILES * len(streams) - 1
-            x_waiting = []
-            for j in range(HID_BANKS):
-                waiting = w_step(next_pair + j, waiting, ready)
-                quantise_x(x_waiting)
-                x_waiting = [x_pass(before[0], before[1], j)]
-                ready = multiply_ready(ready, 2 * HID_BANKS + j)
-            quantise_x(x_waiting)
-            next_pair = next_pair + HID_BANKS
+            late_groups = [(st, g) for st in streams[1:] for g in range(st["groups"])]
+            quantise_input(stream_a, 0)
+            banks = embed(0)
+            load_w1(W1_BUFS)
+            u_tiles = []
+            stats = []
+            scalars = []
+            z = []
+            x_t = None
+            waiting = []
+            ready = []
+            x_done = 0
+            for t in range(N_SLOTS):
+                xp = t - X_LAG
+                pair = t - W_START
 
-        for pair in range(next_pair, N_PAIRS):
-            waiting = w_step(pair, waiting, ready)
-            ready = multiply_ready(ready, HID_PASSES)
+                x_t_before = x_t
+                x_t = silu_pass(xp, z) if 0 <= xp < X_PASSES else None
+                if t < X_PASSES:
+                    u_tiles.append(copy_out(banks))
+
+                if t < len(late_groups):
+                    quantise_input(late_groups[t][0], late_groups[t][1])
+                if t < 2 * DETER // BANK:
+                    spread_out_gains(t)
+                if t == len(late_groups):
+                    sort_gains()
+
+                regrouped = []
+                if 0 <= pair:
+                    for c in range(2):
+                        grouped = w_grouped_pool.tile([P, BLK, PACK], BF16, name="w_grouped", align_bytes=64)
+                        regroup(nc.vector.tensor_copy if c == 0 else nc.scalar.copy, grouped[:], w_raw[pair][:, c, :, :])
+                        regrouped.append((grouped, pair_place(pair, c)[0], pair_place(pair, c)[1]))
+                if 0 <= pair + RAW_BUFS < N_PAIRS:
+                    load_w_pair(pair + RAW_BUFS)
+
+                if x_t_before is not None:
+                    x_grouped = xt_pool.tile([P, ROWS, PACK], BF16, name="x_grouped", align_bytes=64)
+                    regroup(nc.vector.tensor_copy, x_grouped[:], x_t_before[:])
+                quantise_w(waiting, ready)
+                waiting = regrouped
+                if 1 <= t <= X_PASSES:
+                    if (t - 1) % HID_BANKS == 0:
+                        stats = [small.tile([P, HID_BANKS, 6], F32, name="stats") for m in range(M_TILES)]
+                    for m in range(M_TILES):
+                        nc.vector.bn_stats(out=stats[m][:, (t - 1) % HID_BANKS, :], in_=u_tiles[t - 1][m][:])
+                    if t % HID_BANKS == 0:
+                        scalars.append([list(norm_scalars(stats[m])) for m in range(M_TILES)])
+                if x_t_before is not None:
+                    quantise_x(xp - 1, x_grouped)
+                    x_done = x_done + 1
+
+                xn = xp + 2
+                if 0 <= xn < X_PASSES:
+                    if xn % HID_BANKS == 0:
+                        mean_var, rstd = scalars[xn // HID_BANKS][1]
+                        shift = small.tile([P, 1], F32, name="shift")
+                        nc.vector.scalar_tensor_tensor(
+                            out=shift[:], in0=mean_var[:, 0:1], scalar=-1.0, in1=rstd[:], op0=ALU.mult, op1=ALU.mult
+                        )
+                        scalars[xn // HID_BANKS][1].append(shift)
+                    normalise(u_tiles[xn], scalars[xn // HID_BANKS])
+                if 0 <= xp + 1 < X_PASSES:
+                    z = transpose_pass(u_tiles[xp + 1])
+                if t + 1 < X_PASSES:
+                    banks = embed(t + 1)
+                if t + 1 + W1_BUFS < X_PASSES:
+                    load_w1(t + 1 + W1_BUFS)
+                ready = multiply_ready(ready, x_done)
+
         quantise_w(waiting, ready)
         while ready:
-            ready = multiply_ready(ready, HID_PASSES)
+            ready = multiply_ready(ready, x_done)
 
         with tc.tile_pool(name="final", bufs=6) as final:
-            scalars = [norm_scalars(out_stats[m]) for m in range(M_TILES)]
+            last = [norm_scalars(out_stats[m]) for m in range(M_TILES)]
             for m in range(M_TILES):
-                mean_var, rstd = scalars[m]
+                mean_var, rstd = last[m]
                 centred = []
                 for g in range(BLOCKS):
                     c_tile = final.tile([P, BLK], F32, name="centred")
@@ -393,11 +427,11 @@ def tile_blockrecurrentmodel_pa_k_kernel(
                     )
                     centred.append(c_tile)
                 for g in range(BLOCKS):
-                    z = final.tile([P, BLK], F32, name="z")
+                    z_tile = final.tile([P, BLK], F32, name="z")
                     nc.vector.scalar_tensor_tensor(
-                        out=z[:], in0=centred[g][:], scalar=rstd[:],
+                        out=z_tile[:], in0=centred[g][:], scalar=rstd[:],
                         in1=out_gain_bias[:, DETER + g * BLK : DETER + (g + 1) * BLK], op0=ALU.mult, op1=ALU.add,
                     )
                     result = final.tile([P, BLK], F32, name="result")
-                    nc.scalar.activation(out=result[:], in_=z[:], func=ACT.Silu)
+                    nc.scalar.activation(out=result[:], in_=z_tile[:], func=ACT.Silu)
                     nc.sync.dma_start(out=out[m * P : (m + 1) * P, g * BLK : (g + 1) * BLK], in_=result[:])

@@ -81,8 +81,6 @@ def tile_blockrecurrentmodel_pa_k_kernel(
 
         ident = consts.tile([P, P], F32, name="ident")
         make_identity(nc, ident[:])
-        ones = consts.tile([P, P], BF16, name="ones")
-        nc.gpsimd.memset(ones[:], 1.0)
         neg_half = consts.tile([P, 1], F32, name="neg_half")
         nc.gpsimd.memset(neg_half[:], -0.5)
         warm = consts.tile([P, 1], F32, name="warm")
@@ -116,9 +114,7 @@ def tile_blockrecurrentmodel_pa_k_kernel(
             planes_s = setup.tile([P, HID], U8, name="planes_s", align_bytes=64)
             planes_d = setup.tile([P, HID], U8, name="planes_d", align_bytes=64)
             vec_rows = setup.tile([P, K_PASS], BF16, name="vec_rows")
-            out_vec_row = setup.tile([P, 2 * DETER], BF16, name="out_vec_row")
             nc.vector.memset(planes_a[:].bitcast(I32), 0)
-            nc.vector.memset(out_vec_row[:], 0.0)
             nc.vector.memset(planes_s[:].bitcast(I32), 0)
             nc.vector.memset(planes_d[:].bitcast(I32), 0)
             nc.vector.memset(vec_rows[:], 0.0)
@@ -188,12 +184,8 @@ def tile_blockrecurrentmodel_pa_k_kernel(
                 load_w1(slot)
             load_input(stream_s)
             load_input(stream_d)
-            for pair in range(RAW_BUFS - W_START):
-                load_w_pair(pair)
             load_scale_rows(planes_s, W_s_scales)
             load_scale_rows(planes_d, W_d_scales)
-            nc.gpsimd.dma_start(out=out_vec_row[0:1, 0:DETER], in_=ln_h_g.rearrange("(o k) -> o k", o=1))
-            nc.gpsimd.dma_start(out=out_vec_row[0:1, DETER:], in_=ln_h_b.rearrange("(o k) -> o k", o=1))
             for v, vec in enumerate([ln_s_g, ln_s_b, ln_a_g, ln_a_b, ln_d_g, ln_d_b]):
                 nc.gpsimd.dma_start(
                     out=vec_rows[HID_BANKS * v : HID_BANKS * (v + 1), :], in_=vec.rearrange("(c k) -> c k", k=K_PASS)
@@ -223,12 +215,6 @@ def tile_blockrecurrentmodel_pa_k_kernel(
                 for t in range(PACK):
                     nc.tensor.transpose(gb_ps[:, t, :], vec_sorted[:, t, :], ident[:])
                 nc.vector.tensor_copy(out=gain_bias[:], in_=gb_ps[:])
-
-            def spread_out_gains(piece):
-                n_cols = slice(piece * BANK, (piece + 1) * BANK)
-                spread = psum_tr.tile([P, BANK], F32, name="spread", tag="tr")
-                nc.tensor.matmul(out=spread[:], lhsT=ones[:], rhs=out_vec_row[:, n_cols], start=True, stop=True)
-                nc.scalar.copy(out=out_gain_bias[:, n_cols], in_=spread[:])
 
             def embed(slot):
                 st = streams[slot // HID_BANKS]
@@ -362,8 +348,6 @@ def tile_blockrecurrentmodel_pa_k_kernel(
 
                 if t < len(late_groups):
                     quantise_input(late_groups[t][0], late_groups[t][1])
-                if t < 2 * DETER // BANK:
-                    spread_out_gains(t)
                 if t == len(late_groups):
                     sort_gains()
 
@@ -391,6 +375,9 @@ def tile_blockrecurrentmodel_pa_k_kernel(
                 if x_t_before is not None:
                     quantise_x(xp - 1, x_grouped)
                     x_done = x_done + 1
+                if t == X_PASSES:
+                    nc.gpsimd.dma_start(out=out_gain_bias[:, 0:DETER], in_=ln_h_g.partition_broadcast(P))
+                    nc.gpsimd.dma_start(out=out_gain_bias[:, DETER:], in_=ln_h_b.partition_broadcast(P))
 
                 xn = xp + 2
                 if 0 <= xn < X_PASSES:

@@ -11,6 +11,7 @@ U8 = mybir.dt.uint8
 FP8X4 = mybir.dt.float8_e4m3fn_x4
 ACT = mybir.ActivationFunctionType
 ALU = mybir.AluOpType
+AXIS = mybir.AxisListType
 
 P = 128
 PACK = 4
@@ -30,12 +31,29 @@ EPS = 1e-3
 
 FLOPS = 2 * ROWS * ((1024 + 512 + 1536) * HID + BLOCKS * HID_PASSES * K_PASS * BLK)
 
-X_LAG = 8
-W_START = 5
-N_SLOTS = W_START + N_PAIRS
+X_START = 2
+X_LAG = 6
+N_SLOTS = max(N_PAIRS, X_START + X_LAG + X_PASSES + 1)
+V_BOTH = 1024
+V_EMB = 896
+V_ACT = 608
+V_NONE = 480
+W_LAG = 1
 RAW_BUFS = 4
-W1_BUFS = 5
+W1_BUFS = 3
 MAX_PASSES_A_SLOT = 4
+
+
+def vector_columns(slot):
+    embeds = 0 <= slot - X_START < X_PASSES
+    activates = 0 <= slot - X_START - X_LAG < X_PASSES
+    if embeds and activates:
+        return V_BOTH
+    if embeds:
+        return V_EMB
+    if activates:
+        return V_ACT
+    return V_NONE
 
 
 def regroup(copy, grouped, planes):
@@ -73,18 +91,18 @@ def tile_blockrecurrentmodel_pa_k_kernel(
         consts = whole.enter_context(tc.tile_pool(name="consts", bufs=1))
         small = whole.enter_context(tc.tile_pool(name="small", bufs=4))
         w_raw_pool = whole.enter_context(tc.tile_pool(name="w_raw", bufs=RAW_BUFS))
-        w_grouped_pool = whole.enter_context(tc.tile_pool(name="w_grouped", bufs=4))
-        w_codes_pool = whole.enter_context(tc.tile_pool(name="w_codes", bufs=14))
+        w_grouped_pool = whole.enter_context(tc.tile_pool(name="w_grouped", bufs=W_LAG + 1))
+        w_codes_pool = whole.enter_context(tc.tile_pool(name="w_codes", bufs=11))
         psum_acc = whole.enter_context(tc.psum_pool(name="psum_acc", bufs=4))
         psum_h = whole.enter_context(tc.psum_pool(name="psum_h", bufs=2))
         psum_tr = whole.enter_context(tc.psum_pool(name="psum_tr", bufs=2))
 
         ident = consts.tile([P, P], F32, name="ident")
         make_identity(nc, ident[:])
-        neg_half = consts.tile([P, 1], F32, name="neg_half")
+        neg_half = consts.tile([P, M_TILES], F32, name="neg_half")
         nc.gpsimd.memset(neg_half[:], -0.5)
         warm = consts.tile([P, 1], F32, name="warm")
-        nc.scalar.activation(out=warm[:], in_=neg_half[:], func=ACT.Silu)
+        nc.scalar.activation(out=warm[:], in_=neg_half[:, 0:1], func=ACT.Silu)
 
         in_codes = consts.tile([P, 6, ROWS], U32, name="in_codes", align_bytes=64)
         in_planes = consts.tile([P, 6, ROWS], U8, name="in_planes", align_bytes=64)
@@ -100,15 +118,16 @@ def tile_blockrecurrentmodel_pa_k_kernel(
             var_eps = small.tile([P, 1], F32, name="var_eps")
             nc.vector.tensor_scalar_add(out=var_eps[:], in0=mean_var[:, 1:2], scalar1=EPS)
             rstd = small.tile([P, 1], F32, name="rstd")
-            nc.gpsimd.tensor_tensor(out=rstd[:], in0=var_eps[:], in1=neg_half[:], op=ALU.pow)
+            nc.gpsimd.tensor_tensor(out=rstd[:], in0=var_eps[:], in1=neg_half[:, 0:1], op=ALU.pow)
             return mean_var, rstd
 
         with ExitStack() as stage1:
             setup = stage1.enter_context(tc.tile_pool(name="setup", bufs=1))
             in_grouped_pool = stage1.enter_context(tc.tile_pool(name="in_grouped", bufs=2))
             w1_pool = stage1.enter_context(tc.tile_pool(name="w1", bufs=W1_BUFS))
-            u_pool = stage1.enter_context(tc.tile_pool(name="u", bufs=18))
-            xt_pool = stage1.enter_context(tc.tile_pool(name="xt", bufs=3))
+            u_pool = stage1.enter_context(tc.tile_pool(name="u", bufs=2 * X_LAG + 2))
+            xt_pool = stage1.enter_context(tc.tile_pool(name="xt", bufs=2))
+            squares_pool = stage1.enter_context(tc.tile_pool(name="squares", bufs=3))
 
             planes_a = setup.tile([P, HID], U8, name="planes_a", align_bytes=64)
             planes_s = setup.tile([P, HID], U8, name="planes_s", align_bytes=64)
@@ -119,11 +138,11 @@ def tile_blockrecurrentmodel_pa_k_kernel(
             nc.vector.memset(planes_d[:].bitcast(I32), 0)
             nc.vector.memset(vec_rows[:], 0.0)
 
-            stream_a = dict(x=a, groups=1, words=W_a_words, first_group=2, planes=planes_a,
+            stream_a = dict(x_sb=[], x=a, groups=1, words=W_a_words, first_group=2, planes=planes_a,
                             gain_row=10, bias_row=15, first_pass=5)
-            stream_s = dict(x=s, groups=2, words=W_s_words, first_group=0, planes=planes_s,
+            stream_s = dict(x_sb=[], x=s, groups=2, words=W_s_words, first_group=0, planes=planes_s,
                             gain_row=0, bias_row=5, first_pass=0)
-            stream_d = dict(x=d, groups=3, words=W_d_words, first_group=3, planes=planes_d,
+            stream_d = dict(x_sb=[], x=d, groups=3, words=W_d_words, first_group=3, planes=planes_d,
                             gain_row=20, bias_row=25, first_pass=10)
             streams = [stream_a, stream_s, stream_d]
 
@@ -137,12 +156,13 @@ def tile_blockrecurrentmodel_pa_k_kernel(
                     return pair % 2, 2 * (pair // 2) + c
                 return 2, 2 * (pair - HID_PASSES) + c
 
-            def load_input(st):
-                x_sb = setup.tile([P, M_TILES, st["groups"] * K_PASS], BF16, name="x_sb%d" % st["groups"])
+            def load_input(st, g):
+                x_sb = u_pool.tile([P, M_TILES, K_PASS], BF16, name="x_sb", tag="u")
                 nc.sync.dma_start(
-                    out=x_sb[:], in_=st["x"].flatten_outer_dims().rearrange("(m p) k -> p m k", p=P)
+                    out=x_sb[:],
+                    in_=st["x"].flatten_outer_dims().rearrange("(m p) k -> p m k", p=P)[:, :, g * K_PASS : (g + 1) * K_PASS],
                 )
-                st["x_sb"] = x_sb
+                st["x_sb"].append(x_sb)
 
             def load_scale_rows(planes, scales):
                 n_rows = 4 * scales.shape[0]
@@ -178,31 +198,38 @@ def tile_blockrecurrentmodel_pa_k_kernel(
                     )
                 w_raw.append(raw)
 
-            load_input(stream_a)
+            load_w_pair(0)
+            load_input(stream_a, 0)
             load_scale_rows(planes_a, W_a_scales)
-            for slot in range(W1_BUFS):
-                load_w1(slot)
-            load_input(stream_s)
-            load_input(stream_d)
+            load_w_pair(1)
+            load_w1(0)
+            load_w_pair(2)
+            load_w1(1)
+            load_w_pair(3)
+            load_w1(2)
+            for g in range(2):
+                load_input(stream_s, g)
             load_scale_rows(planes_s, W_s_scales)
-            load_scale_rows(planes_d, W_d_scales)
             for v, vec in enumerate([ln_s_g, ln_s_b, ln_a_g, ln_a_b, ln_d_g, ln_d_b]):
                 nc.gpsimd.dma_start(
                     out=vec_rows[HID_BANKS * v : HID_BANKS * (v + 1), :], in_=vec.rearrange("(c k) -> c k", k=K_PASS)
                 )
 
-            def quantise_input(st, g):
+            def transpose_input(st, g):
                 xt = psum_tr.tile([P, 2, ROWS], F32, name="xt_ps", tag="tr")
                 for half in range(2):
                     for m in range(M_TILES):
-                        words = st["x_sb"][:, m, :].bitcast(F32)
+                        words = st["x_sb"][g][:, m, :].bitcast(F32)
                         nc.tensor.transpose(
-                            xt[:, half, m * P : (m + 1) * P], words[:, 256 * g + half : 256 * (g + 1) : 2], ident[:]
+                            xt[:, half, m * P : (m + 1) * P], words[:, half::2], ident[:]
                         )
                 grouped = in_grouped_pool.tile([P, ROWS * PACK], BF16, name="in_grouped", align_bytes=64)
                 nc.scalar.copy(
                     out=grouped[:].bitcast(F32).rearrange("p (r h) -> p r h", h=2), in_=xt[:].rearrange("p h r -> p r h")
                 )
+                return grouped
+
+            def quantise_input(st, g, grouped):
                 group = st["first_group"] + g
                 nc.vector.quantize_mx(
                     out=in_codes[:, group, :].bitcast(FP8X4), scales=in_planes[:, group, :], in_=grouped[:]
@@ -211,10 +238,13 @@ def tile_blockrecurrentmodel_pa_k_kernel(
             def sort_gains():
                 vec_sorted = setup.tile([P, PACK, P], F32, name="vec_sorted")
                 nc.vector.tensor_copy(out=vec_sorted[:], in_=vec_rows[:].rearrange("r (q t) -> r t q", t=PACK))
+                return vec_sorted
+
+            def transpose_gains(vec_sorted):
                 gb_ps = psum_tr.tile([P, PACK, P], F32, name="gb_ps", tag="tr")
                 for t in range(PACK):
                     nc.tensor.transpose(gb_ps[:, t, :], vec_sorted[:, t, :], ident[:])
-                nc.vector.tensor_copy(out=gain_bias[:], in_=gb_ps[:])
+                return gb_ps
 
             def embed(slot):
                 st = streams[slot // HID_BANKS]
@@ -237,22 +267,71 @@ def tile_blockrecurrentmodel_pa_k_kernel(
                     banks.append(bank)
                 return banks
 
-            def copy_out(banks):
+            def copy_out(banks, sums, j):
                 tiles = []
-                for bank in banks:
-                    u = u_pool.tile([P, PACK, P], F32, name="u")
-                    nc.scalar.copy(out=u[:], in_=bank[:].rearrange("p (q t) -> p t q", t=PACK))
+                for m, bank in enumerate(banks):
+                    u = u_pool.tile([P, PACK, P], F32, name="u", tag="u")
+                    nc.scalar.activation(
+                        out=u[:], in_=bank[:].rearrange("p (q t) -> p t q", t=PACK), func=ACT.Copy,
+                        accum_out=sums[:, 0, m, j : j + 1],
+                    )
                     tiles.append(u)
                 return tiles
 
-            def normalise(tiles, scalars):
-                mean_var, rstd = scalars[0][0], scalars[0][1]
+            def first_means(sums):
+                neg_first = small.tile([P, M_TILES], F32, name="neg_first")
+                nc.scalar.mul(neg_first[:], sums[:, 0, :, 0], -1.0 / BANK)
+                return neg_first
+
+            def sum_squares(tiles, sums, neg_first, j):
+                for m in range(M_TILES):
+                    squares = squares_pool.tile([P, BANK], BF16, name="squares")
+                    nc.scalar.activation(
+                        out=squares[:], in_=tiles[m][:].rearrange("p t q -> p (t q)"), func=ACT.Square,
+                        bias=neg_first[:, m : m + 1], accum_out=sums[:, 1, m, j : j + 1],
+                    )
+
+            def stream_scalars(sums, neg_first):
+                totals = small.tile([P, 2, M_TILES], F32, name="totals")
+                distance = small.tile([P, M_TILES], F32, name="distance")
+                square = small.tile([P, M_TILES], F32, name="square")
+                mean_square = small.tile([P, M_TILES], F32, name="mean_square")
+                var_eps = small.tile([P, M_TILES], F32, name="var_eps2")
+                rstd = small.tile([P, M_TILES], F32, name="rstd2")
+                shift = small.tile([P, M_TILES], F32, name="shift")
+
+                def add_banks():
+                    nc.vector.tensor_reduce(out=totals[:], in_=sums[:], axis=AXIS.X, op=ALU.add)
+
+                def centre():
+                    nc.vector.scalar_tensor_tensor(
+                        out=distance[:], in0=totals[:, 0, :], scalar=1.0 / HID, in1=neg_first[:], op0=ALU.mult, op1=ALU.add
+                    )
+                    nc.vector.tensor_scalar(
+                        out=mean_square[:], in0=totals[:, 1, :], scalar1=1.0 / HID, scalar2=EPS, op0=ALU.mult, op1=ALU.add
+                    )
+
+                def square_distance():
+                    nc.vector.tensor_tensor(out=square[:], in0=distance[:], in1=distance[:], op=ALU.mult)
+
+                def invert():
+                    nc.vector.tensor_tensor(out=var_eps[:], in0=mean_square[:], in1=square[:], op=ALU.subtract)
+                    nc.gpsimd.tensor_tensor(out=rstd[:], in0=var_eps[:], in1=neg_half[:], op=ALU.pow)
+
+                def scale_mean():
+                    nc.vector.scalar_tensor_tensor(
+                        out=shift[:], in0=totals[:, 0, :], scalar=-1.0 / HID, in1=rstd[:], op0=ALU.mult, op1=ALU.mult
+                    )
+
+                return [add_banks, centre, square_distance, invert, scale_mean], rstd, shift
+
+            def normalise(tiles, rstd, shift):
                 nc.vector.tensor_scalar(
-                    out=tiles[0][:], in0=tiles[0][:], scalar1=mean_var[:, 0:1], scalar2=rstd[:],
-                    op0=ALU.subtract, op1=ALU.mult,
+                    out=tiles[0][:], in0=tiles[0][:], scalar1=rstd[:, 0:1], scalar2=shift[:, 0:1],
+                    op0=ALU.mult, op1=ALU.add,
                 )
                 nc.scalar.activation(
-                    out=tiles[1][:], in_=tiles[1][:], func=ACT.Identity, scale=scalars[1][1][:], bias=scalars[1][2][:]
+                    out=tiles[1][:], in_=tiles[1][:], func=ACT.Identity, scale=rstd[:, 1:2], bias=shift[:, 1:2]
                 )
 
             def transpose_pass(tiles):
@@ -286,22 +365,45 @@ def tile_blockrecurrentmodel_pa_k_kernel(
                     in_=x_grouped[:].rearrange("p n t -> p (n t)"),
                 )
 
-            def quantise_w(waiting, ready):
-                for grouped, block, pos in waiting:
-                    codes = w_codes_pool.tile([P, BLK], U32, name="w_codes", align_bytes=64)
-                    plane = w_codes_pool.tile([P, BLK], U8, name="w_plane", align_bytes=64)
-                    nc.vector.quantize_mx(
-                        out=codes[:].bitcast(FP8X4), scales=plane[:], in_=grouped[:].rearrange("p n t -> p (n t)")
-                    )
-                    ready.append((codes, plane, block, pos))
+            def regroup_pair(slot, steps):
+                raw = w_raw[slot]
+                grouped = w_grouped_pool.tile([P, 2 * BLK, PACK], BF16, name="w_grouped", align_bytes=64)
+                v_cols = vector_columns(slot)
+                for copy, lo, hi in [(nc.vector.tensor_copy, 0, v_cols), (nc.scalar.copy, v_cols, 2 * BLK)]:
+                    for c in range(2):
+                        a, b = max(lo, c * BLK), min(hi, (c + 1) * BLK)
+                        if a < b:
+                            regroup(copy, grouped[:, a:b, :], raw[:, c, :, a - c * BLK : b - c * BLK])
+                            if steps and hi == v_cols:
+                                steps.pop(0)()
+                return grouped
+
+            def quantise_w(slot, grouped, ready):
+                codes = w_codes_pool.tile([P, 2, BLK], U32, name="w_codes", align_bytes=64)
+                plane = w_codes_pool.tile([P, 2, BLK], U8, name="w_plane", align_bytes=64)
+                nc.vector.quantize_mx(
+                    out=codes[:].rearrange("p c n -> p (c n)").bitcast(FP8X4),
+                    scales=plane[:].rearrange("p c n -> p (c n)"),
+                    in_=grouped[:].rearrange("p n t -> p (n t)"),
+                )
+                for c in range(2):
+                    block, pos = pair_place(slot, c)
+                    ready.append((codes[:, c, :], plane[:, c, :], block, pos))
 
             acc = [[psum_acc.tile([P, BANK], F32, name="acc") for m in range(M_TILES)] for block in range(2)]
 
-            def multiply_ready(chunks, x_done):
+            multiplied = [0] * BLOCKS
+
+            def multiply_ready(chunks, x_done, banks_free):
                 n = 0
-                while n < min(len(chunks), MAX_PASSES_A_SLOT) and pass_order[chunks[n][3]][1] <= x_done:
-                    codes, plane, block, pos = chunks[n]
+                left = []
+                for chunk in chunks:
+                    codes, plane, block, pos = chunk
                     k_pass = pass_order[pos][0]
+                    if n == MAX_PASSES_A_SLOT or pass_order[pos][1] > x_done or (block == 2 and not banks_free):
+                        left.append(chunk)
+                        continue
+                    n = n + 1
                     if block == len(acc):
                         acc.append([psum_h.tile([P, BANK], F32, name="acc_last", tag="h") for m in range(M_TILES)])
                     for m in range(M_TILES):
@@ -314,23 +416,24 @@ def tile_blockrecurrentmodel_pa_k_kernel(
                             out=acc[block][m][:],
                             lhsT=lhs.bitcast(FP8X4),
                             lhsT_scale=lhs_plane,
-                            rhs=codes[:].bitcast(FP8X4),
-                            rhs_scale=plane[:],
-                            start=(pos == 0),
-                            stop=(pos == HID_PASSES - 1),
+                            rhs=codes.bitcast(FP8X4),
+                            rhs_scale=plane,
+                            start=(multiplied[block] == 0),
+                            stop=(multiplied[block] == HID_PASSES - 1),
                         )
-                    if pos == HID_PASSES - 1:
+                    multiplied[block] = multiplied[block] + 1
+                    if multiplied[block] == HID_PASSES:
                         for m in range(M_TILES):
                             nc.vector.bn_stats(out=out_stats[m][:, block, :], in_=acc[block][m][:])
-                    n = n + 1
-                return chunks[n:]
+                return left
 
-            late_groups = [(st, g) for st in streams[1:] for g in range(st["groups"])]
-            quantise_input(stream_a, 0)
-            banks = embed(0)
-            load_w1(W1_BUFS)
+            late_groups = {-1: (stream_a, 0), 1: (stream_s, 0), 2: (stream_s, 1)}
+            for g in range(3):
+                late_groups[3 + g] = (stream_d, g)
+            banks = None
             u_tiles = []
-            stats = []
+            sums = None
+            neg_first = None
             scalars = []
             z = []
             x_t = None
@@ -338,68 +441,81 @@ def tile_blockrecurrentmodel_pa_k_kernel(
             ready = []
             x_done = 0
             for t in range(N_SLOTS):
-                xp = t - X_LAG
-                pair = t - W_START
+                e = t - X_START
+                xp = e - X_LAG
+
+                steps = []
+                if e % HID_BANKS == 0 and 0 < e <= X_PASSES:
+                    steps, rstd, shift = stream_scalars(sums, neg_first)
+                    scalars.append((rstd, shift))
 
                 x_t_before = x_t
+                if 0 <= xp < X_PASSES:
+                    z = transpose_pass(u_tiles[xp])
+                if 0 <= e < X_PASSES:
+                    if e % HID_BANKS == 0:
+                        sums = small.tile([P, 2, M_TILES, HID_BANKS], F32, name="sums")
+                    u_tiles.append(copy_out(banks, sums, e % HID_BANKS))
+                    if e % HID_BANKS == 0:
+                        neg_first = first_means(sums)
+
+                if e in late_groups:
+                    in_grouped = transpose_input(late_groups[e][0], late_groups[e][1])
+                if e == 3:
+                    vec_sorted = sort_gains()
+                if e == 4:
+                    gb_ps = transpose_gains(vec_sorted)
+                if e == 5:
+                    nc.vector.tensor_copy(out=gain_bias[:], in_=gb_ps[:])
+
+                ready = multiply_ready(ready, x_done, e >= X_PASSES)
+
+                if t < N_PAIRS:
+                    waiting.append((t, regroup_pair(t, steps)))
+                if t + RAW_BUFS < N_PAIRS:
+                    load_w_pair(t + RAW_BUFS)
+
                 x_t = silu_pass(xp, z) if 0 <= xp < X_PASSES else None
-                if t < X_PASSES:
-                    u_tiles.append(copy_out(banks))
-
-                if t < len(late_groups):
-                    quantise_input(late_groups[t][0], late_groups[t][1])
-                if t == len(late_groups):
-                    sort_gains()
-
-                regrouped = []
-                if 0 <= pair:
-                    for c in range(2):
-                        grouped = w_grouped_pool.tile([P, BLK, PACK], BF16, name="w_grouped", align_bytes=64)
-                        regroup(nc.vector.tensor_copy if c == 0 else nc.scalar.copy, grouped[:], w_raw[pair][:, c, :, :])
-                        regrouped.append((grouped, pair_place(pair, c)[0], pair_place(pair, c)[1]))
-                if 0 <= pair + RAW_BUFS < N_PAIRS:
-                    load_w_pair(pair + RAW_BUFS)
 
                 if x_t_before is not None:
                     x_grouped = xt_pool.tile([P, ROWS, PACK], BF16, name="x_grouped", align_bytes=64)
                     regroup(nc.vector.tensor_copy, x_grouped[:], x_t_before[:])
-                quantise_w(waiting, ready)
-                waiting = regrouped
-                if 1 <= t <= X_PASSES:
-                    if (t - 1) % HID_BANKS == 0:
-                        stats = [small.tile([P, HID_BANKS, 6], F32, name="stats") for m in range(M_TILES)]
-                    for m in range(M_TILES):
-                        nc.vector.bn_stats(out=stats[m][:, (t - 1) % HID_BANKS, :], in_=u_tiles[t - 1][m][:])
-                    if t % HID_BANKS == 0:
-                        scalars.append([list(norm_scalars(stats[m])) for m in range(M_TILES)])
+                    if steps:
+                        steps.pop(0)()
+                if waiting and waiting[0][0] <= t - W_LAG:
+                    quantise_w(waiting[0][0], waiting[0][1], ready)
+                    waiting = waiting[1:]
+                    if steps:
+                        steps.pop(0)()
+                if 0 <= e < X_PASSES:
+                    sum_squares(u_tiles[e], sums, neg_first, e % HID_BANKS)
                 if x_t_before is not None:
                     quantise_x(xp - 1, x_grouped)
                     x_done = x_done + 1
-                if t == X_PASSES:
+                for step in steps:
+                    step()
+                if e in late_groups:
+                    quantise_input(late_groups[e][0], late_groups[e][1], in_grouped)
+                if e == 0:
+                    for g in range(3):
+                        load_input(stream_d, g)
+                    load_scale_rows(planes_d, W_d_scales)
+                if e == X_PASSES:
                     nc.gpsimd.dma_start(out=out_gain_bias[:, 0:DETER], in_=ln_h_g.partition_broadcast(P))
                     nc.gpsimd.dma_start(out=out_gain_bias[:, DETER:], in_=ln_h_b.partition_broadcast(P))
 
-                xn = xp + 2
+                xn = xp + 1
                 if 0 <= xn < X_PASSES:
-                    if xn % HID_BANKS == 0:
-                        mean_var, rstd = scalars[xn // HID_BANKS][1]
-                        shift = small.tile([P, 1], F32, name="shift")
-                        nc.vector.scalar_tensor_tensor(
-                            out=shift[:], in0=mean_var[:, 0:1], scalar=-1.0, in1=rstd[:], op0=ALU.mult, op1=ALU.mult
-                        )
-                        scalars[xn // HID_BANKS][1].append(shift)
-                    normalise(u_tiles[xn], scalars[xn // HID_BANKS])
-                if 0 <= xp + 1 < X_PASSES:
-                    z = transpose_pass(u_tiles[xp + 1])
-                if t + 1 < X_PASSES:
-                    banks = embed(t + 1)
-                if t + 1 + W1_BUFS < X_PASSES:
-                    load_w1(t + 1 + W1_BUFS)
-                ready = multiply_ready(ready, x_done)
+                    normalise(u_tiles[xn], scalars[xn // HID_BANKS][0], scalars[xn // HID_BANKS][1])
+                if 0 <= e + 1 < X_PASSES:
+                    banks = embed(e + 1)
+                    if e + 1 + W1_BUFS < X_PASSES:
+                        load_w1(e + 1 + W1_BUFS)
 
-        quantise_w(waiting, ready)
-        while ready:
-            ready = multiply_ready(ready, x_done)
+            for slot, grouped in waiting:
+                quantise_w(slot, grouped, ready)
+            while ready:
+                ready = multiply_ready(ready, x_done, True)
 
         with tc.tile_pool(name="final", bufs=6) as final:
             last = [norm_scalars(out_stats[m]) for m in range(M_TILES)]

@@ -39,6 +39,7 @@ V_EMB = 896
 V_ACT = 608
 V_NONE = 480
 W_LAG = 1
+RUN = 8
 RAW_BUFS = 4
 W1_BUFS = 3
 MAX_PASSES_A_SLOT = 4
@@ -58,8 +59,8 @@ def vector_columns(slot):
 
 def regroup(copy, grouped, planes):
     copy(
-        out=grouped.rearrange("p (c i) t -> p c t i", i=4),
-        in_=planes.rearrange("p t (c i) -> p c t i", i=4),
+        out=grouped.rearrange("p (c i) t -> p c t i", i=RUN),
+        in_=planes.rearrange("p t (c i) -> p c t i", i=RUN),
     )
 
 

@@ -212,7 +212,7 @@ def tile_blockrecurrentmodel_pa_k_kernel(
                 load_input(stream_s, g)
             load_scale_rows(planes_s, W_s_scales)
             for v, vec in enumerate([ln_s_g, ln_s_b, ln_a_g, ln_a_b, ln_d_g, ln_d_b]):
-                nc.gpsimd.dma_start(
+                nc.scalar.dma_start(
                     out=vec_rows[HID_BANKS * v : HID_BANKS * (v + 1), :], in_=vec.rearrange("(c k) -> c k", k=K_PASS)
                 )
 
@@ -501,9 +501,9 @@ def tile_blockrecurrentmodel_pa_k_kernel(
                     for g in range(3):
                         load_input(stream_d, g)
                     load_scale_rows(planes_d, W_d_scales)
-                if e == X_PASSES:
-                    nc.gpsimd.dma_start(out=out_gain_bias[:, 0:DETER], in_=ln_h_g.partition_broadcast(P))
-                    nc.gpsimd.dma_start(out=out_gain_bias[:, DETER:], in_=ln_h_b.partition_broadcast(P))
+                if t == N_PAIRS - RAW_BUFS:
+                    nc.sync.dma_start(out=out_gain_bias[:, 0:DETER], in_=ln_h_g.partition_broadcast(P))
+                    nc.sync.dma_start(out=out_gain_bias[:, DETER:], in_=ln_h_b.partition_broadcast(P))
 
                 xn = xp + 1
                 if 0 <= xn < X_PASSES:

@@ -134,10 +134,10 @@ def tile_blockrecurrentmodel_pa_k_kernel(
             planes_s = setup.tile([P, HID], U8, name="planes_s", align_bytes=64)
             planes_d = setup.tile([P, HID], U8, name="planes_d", align_bytes=64)
             vec_rows = setup.tile([P, K_PASS], BF16, name="vec_rows")
+            nc.vector.memset(vec_rows[:], 0.0)
             nc.vector.memset(planes_a[:].bitcast(I32), 0)
             nc.vector.memset(planes_s[:].bitcast(I32), 0)
             nc.vector.memset(planes_d[:].bitcast(I32), 0)
-            nc.vector.memset(vec_rows[:], 0.0)
 
             stream_a = dict(x_sb=[], x=a, groups=1, words=W_a_words, first_group=2, planes=planes_a,
                             gain_row=10, bias_row=15, first_pass=5)
@@ -212,7 +212,7 @@ def tile_blockrecurrentmodel_pa_k_kernel(
                 load_input(stream_s, g)
             load_scale_rows(planes_s, W_s_scales)
             for v, vec in enumerate([ln_s_g, ln_s_b, ln_a_g, ln_a_b, ln_d_g, ln_d_b]):
-                nc.scalar.dma_start(
+                nc.gpsimd.dma_start(
                     out=vec_rows[HID_BANKS * v : HID_BANKS * (v + 1), :], in_=vec.rearrange("(c k) -> c k", k=K_PASS)
                 )
 

@@ -34,9 +34,9 @@ FLOPS = 2 * ROWS * ((1024 + 512 + 1536) * HID + BLOCKS * HID_PASSES * K_PASS * B
 X_START = 2
 X_LAG = 6
 N_SLOTS = max(N_PAIRS, X_START + X_LAG + X_PASSES + 1)
-V_BOTH = 1024
+V_BOTH = 960
 V_EMB = 896
-V_ACT = 608
+V_ACT = 544
 V_NONE = 480
 W_LAG = 1
 RUN = 8

@@ -40,8 +40,9 @@ V_ACT = 544
 V_NONE = 480
 W_LAG = 1
 RUN = 8
+AHEAD = 3
 RAW_BUFS = 4
-W1_BUFS = 3
+W1_BUFS = 4
 MAX_PASSES_A_SLOT = 4
 
 
@@ -139,11 +140,11 @@ def tile_blockrecurrentmodel_pa_k_kernel(
             nc.vector.memset(planes_s[:].bitcast(I32), 0)
             nc.vector.memset(planes_d[:].bitcast(I32), 0)
 
-            stream_a = dict(x_sb=[], x=a, groups=1, words=W_a_words, first_group=2, planes=planes_a,
+            stream_a = dict(x_sb=[], x=a, groups=1, words=W_a_words, first_group=2, planes=planes_a, scales=W_a_scales,
                             gain_row=10, bias_row=15, first_pass=5)
-            stream_s = dict(x_sb=[], x=s, groups=2, words=W_s_words, first_group=0, planes=planes_s,
+            stream_s = dict(x_sb=[], x=s, groups=2, words=W_s_words, first_group=0, planes=planes_s, scales=W_s_scales,
                             gain_row=0, bias_row=5, first_pass=0)
-            stream_d = dict(x_sb=[], x=d, groups=3, words=W_d_words, first_group=3, planes=planes_d,
+            stream_d = dict(x_sb=[], x=d, groups=3, words=W_d_words, first_group=3, planes=planes_d, scales=W_d_scales,
                             gain_row=20, bias_row=25, first_pass=10)
             streams = [stream_a, stream_s, stream_d]
 
@@ -165,7 +166,8 @@ def tile_blockrecurrentmodel_pa_k_kernel(
                 )
                 st["x_sb"].append(x_sb)
 
-            def load_scale_rows(planes, scales):
+            def load_scale_rows(st):
+                planes, scales = st["planes"], st["scales"]
                 n_rows = 4 * scales.shape[0]
                 for quad in range(4):
                     nc.sync.dma_start(
@@ -199,18 +201,23 @@ def tile_blockrecurrentmodel_pa_k_kernel(
                     )
                 w_raw.append(raw)
 
-            load_w_pair(0)
-            load_input(stream_a, 0)
-            load_scale_rows(planes_a, W_a_scales)
-            load_w_pair(1)
-            load_w1(0)
-            load_w_pair(2)
-            load_w1(1)
-            load_w_pair(3)
-            load_w1(2)
-            for g in range(2):
-                load_input(stream_s, g)
-            load_scale_rows(planes_s, W_s_scales)
+            late_groups = {-1: (stream_a, 0), 1: (stream_s, 0), 2: (stream_s, 1)}
+            for g in range(3):
+                late_groups[3 + g] = (stream_d, g)
+
+            def load_for(slot):
+                e = slot - X_START
+                if e in late_groups:
+                    load_input(late_groups[e][0], late_groups[e][1])
+                if slot < N_PAIRS:
+                    load_w_pair(slot)
+                if 0 <= e + 1 < X_PASSES:
+                    if (e + 1) % HID_BANKS == 0:
+                        load_scale_rows(streams[(e + 1) // HID_BANKS])
+                    load_w1(e + 1)
+
+            for slot in range(AHEAD):
+                load_for(slot)
             for v, vec in enumerate([ln_s_g, ln_s_b, ln_a_g, ln_a_b, ln_d_g, ln_d_b]):
                 nc.gpsimd.dma_start(
                     out=vec_rows[HID_BANKS * v : HID_BANKS * (v + 1), :], in_=vec.rearrange("(c k) -> c k", k=K_PASS)
@@ -428,9 +435,6 @@ def tile_blockrecurrentmodel_pa_k_kernel(
                             nc.vector.bn_stats(out=out_stats[m][:, block, :], in_=acc[block][m][:])
                 return left
 
-            late_groups = {-1: (stream_a, 0), 1: (stream_s, 0), 2: (stream_s, 1)}
-            for g in range(3):
-                late_groups[3 + g] = (stream_d, g)
             banks = None
             u_tiles = []
             sums = None
@@ -473,8 +477,7 @@ def tile_blockrecurrentmodel_pa_k_kernel(
 
                 if t < N_PAIRS:
                     waiting.append((t, regroup_pair(t, steps)))
-                if t + RAW_BUFS < N_PAIRS:
-                    load_w_pair(t + RAW_BUFS)
+                load_for(t + AHEAD)
 
                 x_t = silu_pass(xp, z) if 0 <= xp < X_PASSES else None
 
@@ -497,11 +500,7 @@ def tile_blockrecurrentmodel_pa_k_kernel(
                     step()
                 if e in late_groups:
                     quantise_input(late_groups[e][0], late_groups[e][1], in_grouped)
-                if e == 0:
-                    for g in range(3):
-                        load_input(stream_d, g)
-                    load_scale_rows(planes_d, W_d_scales)
-                if t == N_PAIRS - RAW_BUFS:
+                if t == N_PAIRS - AHEAD:
                     nc.sync.dma_start(out=out_gain_bias[:, 0:DETER], in_=ln_h_g.partition_broadcast(P))
                     nc.sync.dma_start(out=out_gain_bias[:, DETER:], in_=ln_h_b.partition_broadcast(P))
 
@@ -510,8 +509,6 @@ def tile_blockrecurrentmodel_pa_k_kernel(
                     normalise(u_tiles[xn], scalars[xn // HID_BANKS][0], scalars[xn // HID_BANKS][1])
                 if 0 <= e + 1 < X_PASSES:
                     banks = embed(e + 1)
-                    if e + 1 + W1_BUFS < X_PASSES:
-                        load_w1(e + 1 + W1_BUFS)
 
             for slot, grouped in waiting:
                 quantise_w(slot, grouped, ready)

@@ -35,7 +35,7 @@ X_START = 2
 X_LAG = 6
 N_SLOTS = max(N_PAIRS, X_START + X_LAG + X_PASSES + 1)
 V_BOTH = 960
-V_EMB = 896
+V_EMB = 832
 V_ACT = 544
 V_NONE = 480
 W_LAG = 1
@@ -127,7 +127,7 @@ def tile_blockrecurrentmodel_pa_k_kernel(
             setup = stage1.enter_context(tc.tile_pool(name="setup", bufs=1))
             in_grouped_pool = stage1.enter_context(tc.tile_pool(name="in_grouped", bufs=2))
             w1_pool = stage1.enter_context(tc.tile_pool(name="w1", bufs=W1_BUFS))
-            u_pool = stage1.enter_context(tc.tile_pool(name="u", bufs=2 * X_LAG + 2))
+            u_pool = stage1.enter_context(tc.tile_pool(name="u", bufs=2 * X_LAG + 3))
             xt_pool = stage1.enter_context(tc.tile_pool(name="xt", bufs=2))
             squares_pool = stage1.enter_context(tc.tile_pool(name="squares", bufs=3))
 
@@ -149,7 +149,7 @@ def tile_blockrecurrentmodel_pa_k_kernel(
             streams = [stream_a, stream_s, stream_d]
 
             pass_order = [(1 + stream_a["first_pass"] + j, 1 + j) for j in range(HID_BANKS)]
-            pass_order.append((0, 0))
+            pass_order.append((0, HID_BANKS))
             pass_order.extend([(1 + stream_s["first_pass"] + j, HID_BANKS + 1 + j) for j in range(HID_BANKS)])
             pass_order.extend([(1 + stream_d["first_pass"] + j, 2 * HID_BANKS + 1 + j) for j in range(HID_BANKS)])
 
@@ -201,9 +201,9 @@ def tile_blockrecurrentmodel_pa_k_kernel(
                     )
                 w_raw.append(raw)
 
-            late_groups = {-1: (stream_a, 0), 1: (stream_s, 0), 2: (stream_s, 1)}
+            late_groups = {-1: (stream_a, 0), 2: (stream_s, 0), 3: (stream_s, 1)}
             for g in range(3):
-                late_groups[3 + g] = (stream_d, g)
+                late_groups[6 + g] = (stream_d, g)
 
             def load_for(slot):
                 e = slot - X_START
@@ -455,6 +455,8 @@ def tile_blockrecurrentmodel_pa_k_kernel(
                     scalars.append((rstd, shift))
 
                 x_t_before = x_t
+                if e in late_groups:
+                    in_grouped = transpose_input(late_groups[e][0], late_groups[e][1])
                 if 0 <= xp < X_PASSES:
                     z = transpose_pass(u_tiles[xp])
                 if 0 <= e < X_PASSES:
@@ -463,9 +465,9 @@ def tile_blockrecurrentmodel_pa_k_kernel(
                     u_tiles.append(copy_out(banks, sums, e % HID_BANKS))
                     if e % HID_BANKS == 0:
                         neg_first = first_means(sums)
+                    if e % HID_BANKS == HID_BANKS - 1:
+                        sum_squares(u_tiles[e], sums, neg_first, e % HID_BANKS)
 
-                if e in late_groups:
-                    in_grouped = transpose_input(late_groups[e][0], late_groups[e][1])
                 if e == 3:
                     vec_sorted = sort_gains()
                 if e == 4:
@@ -475,6 +477,10 @@ def tile_blockrecurrentmodel_pa_k_kernel(
 
                 ready = multiply_ready(ready, x_done, e >= X_PASSES)
 
+                if steps:
+                    steps.pop(0)()
+                    if x_t_before is None:
+                        steps.pop(0)()
                 if t < N_PAIRS:
                     waiting.append((t, regroup_pair(t, steps)))
                 load_for(t + AHEAD)
@@ -491,7 +497,7 @@ def tile_blockrecurrentmodel_pa_k_kernel(
                     waiting = waiting[1:]
                     if steps:
                         steps.pop(0)()
-                if 0 <= e < X_PASSES:
+                if 0 <= e < X_PASSES and e % HID_BANKS != HID_BANKS - 1:
                     sum_squares(u_tiles[e], sums, neg_first, e % HID_BANKS)
                 if x_t_before is not None:
                     quantise_x(xp - 1, x_grouped)

@@ -101,6 +101,8 @@ def tile_blockrecurrentmodel_pa_k_kernel(
 
         ident = consts.tile([P, P], F32, name="ident")
         make_identity(nc, ident[:])
+        ident_bf = consts.tile([P, P], BF16, name="ident_bf")
+        make_identity(nc, ident_bf[:])
         neg_half = consts.tile([P, M_TILES], F32, name="neg_half")
         nc.gpsimd.memset(neg_half[:], -0.5)
         warm = consts.tile([P, 1], F32, name="warm")
@@ -113,15 +115,6 @@ def tile_blockrecurrentmodel_pa_k_kernel(
         gain_bias = consts.tile([P, PACK, P], F32, name="gain_bias")
         out_gain_bias = consts.tile([P, 2 * DETER], BF16, name="out_gain_bias")
         out_stats = [consts.tile([P, BLOCKS, 6], F32, name="out_stats%d" % m) for m in range(M_TILES)]
-
-        def norm_scalars(stats):
-            mean_var = small.tile([P, 2], F32, name="mean_var")
-            nc.vector.bn_aggr(out=mean_var[:], in_=stats[:].rearrange("p a b -> p (a b)"))
-            var_eps = small.tile([P, 1], F32, name="var_eps")
-            nc.vector.tensor_scalar_add(out=var_eps[:], in0=mean_var[:, 1:2], scalar1=EPS)
-            rstd = small.tile([P, 1], F32, name="rstd")
-            nc.gpsimd.tensor_tensor(out=rstd[:], in0=var_eps[:], in1=neg_half[:, 0:1], op=ALU.pow)
-            return mean_var, rstd
 
         with ExitStack() as stage1:
             setup = stage1.enter_context(tc.tile_pool(name="setup", bufs=1))
@@ -463,8 +456,6 @@ def tile_blockrecurrentmodel_pa_k_kernel(
                     if e % HID_BANKS == 0:
                         sums = small.tile([P, 2, M_TILES, HID_BANKS], F32, name="sums")
                     u_tiles.append(copy_out(banks, sums, e % HID_BANKS))
-                    if e % HID_BANKS == 0:
-                        neg_first = first_means(sums)
                     if e % HID_BANKS == HID_BANKS - 1:
                         sum_squares(u_tiles[e], sums, neg_first, e % HID_BANKS)
 
@@ -483,6 +474,8 @@ def tile_blockrecurrentmodel_pa_k_kernel(
                         steps.pop(0)()
                 if t < N_PAIRS:
                     waiting.append((t, regroup_pair(t, steps)))
+                if 0 <= e < X_PASSES and e % HID_BANKS == 0:
+                    neg_first = first_means(sums)
                 load_for(t + AHEAD)
 
                 x_t = silu_pass(xp, z) if 0 <= xp < X_PASSES else None
@@ -522,23 +515,58 @@ def tile_blockrecurrentmodel_pa_k_kernel(
                 ready = multiply_ready(ready, x_done, True)
 
         with tc.tile_pool(name="final", bufs=6) as final:
-            last = [norm_scalars(out_stats[m]) for m in range(M_TILES)]
+            mean_var = small.tile([P, M_TILES, 2], F32, name="mean_var")
             for m in range(M_TILES):
-                mean_var, rstd = last[m]
-                centred = []
-                for g in range(BLOCKS):
-                    c_tile = final.tile([P, BLK], F32, name="centred")
-                    nc.vector.scalar_tensor_tensor(
-                        out=c_tile[:], in0=acc[g][m][:], scalar=mean_var[:, 0:1],
-                        in1=out_gain_bias[:, g * BLK : (g + 1) * BLK], op0=ALU.subtract, op1=ALU.mult,
-                    )
-                    centred.append(c_tile)
-                for g in range(BLOCKS):
-                    z_tile = final.tile([P, BLK], F32, name="z")
-                    nc.vector.scalar_tensor_tensor(
-                        out=z_tile[:], in0=centred[g][:], scalar=rstd[:],
-                        in1=out_gain_bias[:, DETER + g * BLK : DETER + (g + 1) * BLK], op0=ALU.mult, op1=ALU.add,
-                    )
-                    result = final.tile([P, BLK], F32, name="result")
-                    nc.scalar.activation(out=result[:], in_=z_tile[:], func=ACT.Silu)
-                    nc.sync.dma_start(out=out[m * P : (m + 1) * P, g * BLK : (g + 1) * BLK], in_=result[:])
+                nc.vector.bn_aggr(out=mean_var[:, m, :], in_=out_stats[m][:].rearrange("p a b -> p (a b)"))
+            units = [(m, g) for m in range(M_TILES) for g in range(BLOCKS)]
+            centred = []
+
+            def centre():
+                m, g = units[len(centred)]
+                c_tile = final.tile([P, BLK], F32, name="centred")
+                nc.vector.scalar_tensor_tensor(
+                    out=c_tile[:], in0=acc[g][m][:], scalar=mean_var[:, m, 0:1],
+                    in1=out_gain_bias[:, g * BLK : (g + 1) * BLK], op0=ALU.subtract, op1=ALU.mult,
+                )
+                centred.append(c_tile)
+
+            z_banks = []
+            for n in range(1):
+                bank = psum_tr.tile([P, BLK], F32, name="z_bank", tag="tr")
+                g = units[n][1]
+                nc.tensor.matmul(
+                    bank[:], ident_bf[:], out_gain_bias[:, DETER + g * BLK : DETER + (g + 1) * BLK], start=True, stop=False
+                )
+                z_banks.append(bank)
+
+            centre()
+            var_eps = small.tile([P, M_TILES], F32, name="var_eps")
+            nc.vector.tensor_scalar_add(out=var_eps[:], in0=mean_var[:, :, 1], scalar1=EPS)
+            rstd = small.tile([P, M_TILES], F32, name="rstd")
+            nc.gpsimd.tensor_tensor(out=rstd[:], in0=var_eps[:], in1=neg_half[:], op=ALU.pow)
+            diagonal = final.tile([P, P], F32, name="diagonal")
+            nc.scalar.activation(out=diagonal[:], in_=ident[:], func=ACT.Copy, scale=rstd[:, 0:1])
+            for n in range(1, 1):
+                centre()
+            for n in range(1):
+                nc.tensor.matmul(z_banks[n][:], diagonal[:], centred[n][:], start=False, stop=True)
+
+            def finish(n, z):
+                m, g = units[n]
+                result = final.tile([P, BLK], F32, name="result")
+                nc.scalar.activation(out=result[:], in_=z, func=ACT.Silu)
+                nc.sync.dma_start(out=out[m * P : (m + 1) * P, g * BLK : (g + 1) * BLK], in_=result[:])
+
+            centre()
+            for n in range(1, len(units)):
+                if len(centred) < len(units):
+                    centre()
+                m, g = units[n]
+                z_tile = final.tile([P, BLK], F32, name="z")
+                nc.vector.scalar_tensor_tensor(
+                    out=z_tile[:], in0=centred[n][:], scalar=rstd[:, m : m + 1],
+                    in1=out_gain_bias[:, DETER + g * BLK : DETER + (g + 1) * BLK], op0=ALU.mult, op1=ALU.add,
+                )
+                finish(n, z_tile[:])
+                if n == 2:
+                    finish(0, z_banks[0][:])

from contextlib import ExitStack

import concourse.mybir as mybir
from concourse.masks import make_identity

F32 = mybir.dt.float32
BF16 = mybir.dt.bfloat16
I32 = mybir.dt.int32
U32 = mybir.dt.uint32
U8 = mybir.dt.uint8
FP8X4 = mybir.dt.float8_e4m3fn_x4
ACT = mybir.ActivationFunctionType
ALU = mybir.AluOpType
AXIS = mybir.AxisListType

P = 128
PACK = 4
K_PASS = P * PACK
BANK = 512
ROWS = 256
M_TILES = ROWS // P
HID = 2560
HID_BANKS = HID // BANK
DETER = 1536
BLOCKS = 3
BLK = DETER // BLOCKS
X_PASSES = 3 * HID_BANKS
HID_PASSES = 1 + X_PASSES
N_PAIRS = BLOCKS * HID_PASSES // 2
EPS = 1e-3

FLOPS = 2 * ROWS * ((1024 + 512 + 1536) * HID + BLOCKS * HID_PASSES * K_PASS * BLK)

X_START = 2
X_LAG = 6
N_SLOTS = max(N_PAIRS, X_START + X_LAG + X_PASSES + 1)
V_BOTH = 960
V_EMB = 832
V_ACT = 544
V_NONE = 480
W_LAG = 1
RUN = 8
AHEAD = 3
RAW_BUFS = 4
W1_BUFS = 4
MAX_PASSES_A_SLOT = 4


def vector_columns(slot):
    embeds = 0 <= slot - X_START < X_PASSES
    activates = 0 <= slot - X_START - X_LAG < X_PASSES
    if embeds and activates:
        return V_BOTH
    if embeds:
        return V_EMB
    if activates:
        return V_ACT
    return V_NONE


def regroup(copy, grouped, planes):
    copy(
        out=grouped.rearrange("p (c i) t -> p c t i", i=RUN),
        in_=planes.rearrange("p t (c i) -> p c t i", i=RUN),
    )


def tile_blockrecurrentmodel_pa_k_kernel(
    tc,
    s,
    a,
    d,
    W_s_words,
    W_s_scales,
    W_a_words,
    W_a_scales,
    W_d_words,
    W_d_scales,
    ln_s_g,
    ln_s_b,
    ln_a_g,
    ln_a_b,
    ln_d_g,
    ln_d_b,
    W_hid,
    ln_h_g,
    ln_h_b,
    out,
):
    nc = tc.nc
    with ExitStack() as whole:
        whole.enter_context(tc.manual_schedule())
        consts = whole.enter_context(tc.tile_pool(name="consts", bufs=1))
        small = whole.enter_context(tc.tile_pool(name="small", bufs=4))
        w_raw_pool = whole.enter_context(tc.tile_pool(name="w_raw", bufs=RAW_BUFS))
        w_grouped_pool = whole.enter_context(tc.tile_pool(name="w_grouped", bufs=W_LAG + 1))
        w_codes_pool = whole.enter_context(tc.tile_pool(name="w_codes", bufs=11))
        psum_acc = whole.enter_context(tc.psum_pool(name="psum_acc", bufs=4))
        psum_h = whole.enter_context(tc.psum_pool(name="psum_h", bufs=2))
        psum_tr = whole.enter_context(tc.psum_pool(name="psum_tr", bufs=2))

        ident = consts.tile([P, P], F32, name="ident")
        make_identity(nc, ident[:])
        ident_bf = consts.tile([P, P], BF16, name="ident_bf")
        make_identity(nc, ident_bf[:])
        neg_half = consts.tile([P, M_TILES], F32, name="neg_half")
        nc.gpsimd.memset(neg_half[:], -0.5)
        warm = consts.tile([P, 1], F32, name="warm")
        nc.scalar.activation(out=warm[:], in_=neg_half[:, 0:1], func=ACT.Silu)

        in_codes = consts.tile([P, 6, ROWS], U32, name="in_codes", align_bytes=64)
        in_planes = consts.tile([P, 6, ROWS], U8, name="in_planes", align_bytes=64)
        x_codes = consts.tile([P, X_PASSES, ROWS], U32, name="x_codes", align_bytes=64)
        x_planes = consts.tile([P, X_PASSES, ROWS], U8, name="x_planes", align_bytes=64)
        gain_bias = consts.tile([P, PACK, P], F32, name="gain_bias")
        out_gain_bias = consts.tile([P, 2 * DETER], BF16, name="out_gain_bias")
        out_stats = [consts.tile([P, BLOCKS, 6], F32, name="out_stats%d" % m) for m in range(M_TILES)]

        with ExitStack() as stage1:
            setup = stage1.enter_context(tc.tile_pool(name="setup", bufs=1))
            in_grouped_pool = stage1.enter_context(tc.tile_pool(name="in_grouped", bufs=2))
            w1_pool = stage1.enter_context(tc.tile_pool(name="w1", bufs=W1_BUFS))
            u_pool = stage1.enter_context(tc.tile_pool(name="u", bufs=2 * X_LAG + 3))
            xt_pool = stage1.enter_context(tc.tile_pool(name="xt", bufs=2))
            squares_pool = stage1.enter_context(tc.tile_pool(name="squares", bufs=3))

            planes_a = setup.tile([P, HID], U8, name="planes_a", align_bytes=64)
            planes_s = setup.tile([P, HID], U8, name="planes_s", align_bytes=64)
            planes_d = setup.tile([P, HID], U8, name="planes_d", align_bytes=64)
            vec_rows = setup.tile([P, K_PASS], BF16, name="vec_rows")
            nc.vector.memset(vec_rows[:], 0.0)
            nc.vector.memset(planes_a[:].bitcast(I32), 0)
            nc.vector.memset(planes_s[:].bitcast(I32), 0)
            nc.vector.memset(planes_d[:].bitcast(I32), 0)

            stream_a = dict(x_sb=[], x=a, groups=1, words=W_a_words, first_group=2, planes=planes_a, scales=W_a_scales,
                            gain_row=10, bias_row=15, first_pass=5)
            stream_s = dict(x_sb=[], x=s, groups=2, words=W_s_words, first_group=0, planes=planes_s, scales=W_s_scales,
                            gain_row=0, bias_row=5, first_pass=0)
            stream_d = dict(x_sb=[], x=d, groups=3, words=W_d_words, first_group=3, planes=planes_d, scales=W_d_scales,
                            gain_row=20, bias_row=25, first_pass=10)
            streams = [stream_a, stream_s, stream_d]

            pass_order = [(1 + stream_a["first_pass"] + j, 1 + j) for j in range(HID_BANKS)]
            pass_order.append((0, HID_BANKS))
            pass_order.extend([(1 + stream_s["first_pass"] + j, HID_BANKS + 1 + j) for j in range(HID_BANKS)])
            pass_order.extend([(1 + stream_d["first_pass"] + j, 2 * HID_BANKS + 1 + j) for j in range(HID_BANKS)])

            def pair_place(pair, c):
                if pair < HID_PASSES:
                    return pair % 2, 2 * (pair // 2) + c
                return 2, 2 * (pair - HID_PASSES) + c

            def load_input(st, g):
                x_sb = u_pool.tile([P, M_TILES, K_PASS], BF16, name="x_sb", tag="u")
                nc.sync.dma_start(
                    out=x_sb[:],
                    in_=st["x"].flatten_outer_dims().rearrange("(m p) k -> p m k", p=P)[:, :, g * K_PASS : (g + 1) * K_PASS],
                )
                st["x_sb"].append(x_sb)

            def load_scale_rows(st):
                planes, scales = st["planes"], st["scales"]
                n_rows = 4 * scales.shape[0]
                for quad in range(4):
                    nc.sync.dma_start(
                        out=planes[32 * quad : 32 * quad + n_rows, :].bitcast(I32),
                        in_=scales[:, 4 * quad : 4 * quad + 4, :].bitcast(I32),
                    )

            w1 = []

            def load_w1(slot):
                st = streams[slot // HID_BANKS]
                n_bytes = slice((slot % HID_BANKS) * BANK * PACK, (slot % HID_BANKS + 1) * BANK * PACK)
                words = w1_pool.tile([P, 3, BANK], U32, name="w1", align_bytes=64)
                for g in range(st["groups"]):
                    nc.sync.dma_start(
                        out=words[:, g, :].bitcast(I32),
                        in_=st["words"][g].rearrange("p n t -> p (n t)")[:, n_bytes].bitcast(I32),
                    )
                w1.append(words)

            w_raw = []

            def load_w_pair(pair):
                raw = w_raw_pool.tile([P, 2, PACK, BLK], BF16, name="w_raw")
                for c in range(2):
                    block, pos = pair_place(pair, c)
                    first_row = pass_order[pos][0] * K_PASS
                    nc.sync.dma_start(
                        out=raw[:, c, :, :],
                        in_=W_hid[block, first_row : first_row + K_PASS, :].rearrange("(p t) n -> p t n", t=PACK),
                    )
                w_raw.append(raw)

            late_groups = {-1: (stream_a, 0), 2: (stream_s, 0), 3: (stream_s, 1)}
            for g in range(3):
                late_groups[6 + g] = (stream_d, g)

            def load_for(slot):
                e = slot - X_START
                if e in late_groups:
                    load_input(late_groups[e][0], late_groups[e][1])
                if slot < N_PAIRS:
                    load_w_pair(slot)
                if 0 <= e + 1 < X_PASSES:
                    if (e + 1) % HID_BANKS == 0:
                        load_scale_rows(streams[(e + 1) // HID_BANKS])
                    load_w1(e + 1)

            for slot in range(AHEAD):
                load_for(slot)
            for v, vec in enumerate([ln_s_g, ln_s_b, ln_a_g, ln_a_b, ln_d_g, ln_d_b]):
                nc.gpsimd.dma_start(
                    out=vec_rows[HID_BANKS * v : HID_BANKS * (v + 1), :], in_=vec.rearrange("(c k) -> c k", k=K_PASS)
                )

            def transpose_input(st, g):
                xt = psum_tr.tile([P, 2, ROWS], F32, name="xt_ps", tag="tr")
                for half in range(2):
                    for m in range(M_TILES):
                        words = st["x_sb"][g][:, m, :].bitcast(F32)
                        nc.tensor.transpose(
                            xt[:, half, m * P : (m + 1) * P], words[:, half::2], ident[:]
                        )
                grouped = in_grouped_pool.tile([P, ROWS * PACK], BF16, name="in_grouped", align_bytes=64)
                nc.scalar.copy(
                    out=grouped[:].bitcast(F32).rearrange("p (r h) -> p r h", h=2), in_=xt[:].rearrange("p h r -> p r h")
                )
                return grouped

            def quantise_input(st, g, grouped):
                group = st["first_group"] + g
                nc.vector.quantize_mx(
                    out=in_codes[:, group, :].bitcast(FP8X4), scales=in_planes[:, group, :], in_=grouped[:]
                )

            def sort_gains():
                vec_sorted = setup.tile([P, PACK, P], F32, name="vec_sorted")
                nc.vector.tensor_copy(out=vec_sorted[:], in_=vec_rows[:].rearrange("r (q t) -> r t q", t=PACK))
                return vec_sorted

            def transpose_gains(vec_sorted):
                gb_ps = psum_tr.tile([P, PACK, P], F32, name="gb_ps", tag="tr")
                for t in range(PACK):
                    nc.tensor.transpose(gb_ps[:, t, :], vec_sorted[:, t, :], ident[:])
                return gb_ps

            def embed(slot):
                st = streams[slot // HID_BANKS]
                n_cols = slice((slot % HID_BANKS) * BANK, (slot % HID_BANKS + 1) * BANK)
                banks = []
                for m in range(M_TILES):
                    m_cols = slice(m * P, (m + 1) * P)
                    bank = psum_h.tile([P, BANK], F32, name="h", tag="h")
                    for g in range(st["groups"]):
                        group = st["first_group"] + g
                        nc.tensor.matmul_mx(
                            out=bank[:],
                            lhsT=in_codes[:, group, m_cols].bitcast(FP8X4),
                            lhsT_scale=in_planes[:, group, m_cols],
                            rhs=w1[slot][:, g, :].bitcast(FP8X4),
                            rhs_scale=st["planes"][4 * g : P, n_cols],
                            start=(g == 0),
                            stop=(g == st["groups"] - 1),
                        )
                    banks.append(bank)
                return banks

            def copy_out(banks, sums, j):
                tiles = []
                for m, bank in enumerate(banks):
                    u = u_pool.tile([P, PACK, P], F32, name="u", tag="u")
                    nc.scalar.activation(
                        out=u[:], in_=bank[:].rearrange("p (q t) -> p t q", t=PACK), func=ACT.Copy,
                        accum_out=sums[:, 0, m, j : j + 1],
                    )
                    tiles.append(u)
                return tiles

            def first_means(sums):
                neg_first = small.tile([P, M_TILES], F32, name="neg_first")
                nc.scalar.mul(neg_first[:], sums[:, 0, :, 0], -1.0 / BANK)
                return neg_first

            def sum_squares(tiles, sums, neg_first, j):
                for m in range(M_TILES):
                    squares = squares_pool.tile([P, BANK], BF16, name="squares")
                    nc.scalar.activation(
                        out=squares[:], in_=tiles[m][:].rearrange("p t q -> p (t q)"), func=ACT.Square,
                        bias=neg_first[:, m : m + 1], accum_out=sums[:, 1, m, j : j + 1],
                    )

            def stream_scalars(sums, neg_first):
                totals = small.tile([P, 2, M_TILES], F32, name="totals")
                distance = small.tile([P, M_TILES], F32, name="distance")
                square = small.tile([P, M_TILES], F32, name="square")
                mean_square = small.tile([P, M_TILES], F32, name="mean_square")
                var_eps = small.tile([P, M_TILES], F32, name="var_eps2")
                rstd = small.tile([P, M_TILES], F32, name="rstd2")
                shift = small.tile([P, M_TILES], F32, name="shift")

                def add_banks():
                    nc.vector.tensor_reduce(out=totals[:], in_=sums[:], axis=AXIS.X, op=ALU.add)

                def centre():
                    nc.vector.scalar_tensor_tensor(
                        out=distance[:], in0=totals[:, 0, :], scalar=1.0 / HID, in1=neg_first[:], op0=ALU.mult, op1=ALU.add
                    )
                    nc.vector.tensor_scalar(
                        out=mean_square[:], in0=totals[:, 1, :], scalar1=1.0 / HID, scalar2=EPS, op0=ALU.mult, op1=ALU.add
                    )

                def square_distance():
                    nc.vector.tensor_tensor(out=square[:], in0=distance[:], in1=distance[:], op=ALU.mult)

                def invert():
                    nc.vector.tensor_tensor(out=var_eps[:], in0=mean_square[:], in1=square[:], op=ALU.subtract)
                    nc.gpsimd.tensor_tensor(out=rstd[:], in0=var_eps[:], in1=neg_half[:], op=ALU.pow)

                def scale_mean():
                    nc.vector.scalar_tensor_tensor(
                        out=shift[:], in0=totals[:, 0, :], scalar=-1.0 / HID, in1=rstd[:], op0=ALU.mult, op1=ALU.mult
                    )

                return [add_banks, centre, square_distance, invert, scale_mean], rstd, shift

            def normalise(tiles, rstd, shift):
                nc.vector.tensor_scalar(
                    out=tiles[0][:], in0=tiles[0][:], scalar1=rstd[:, 0:1], scalar2=shift[:, 0:1],
                    op0=ALU.mult, op1=ALU.add,
                )
                nc.scalar.activation(
                    out=tiles[1][:], in_=tiles[1][:], func=ACT.Identity, scale=rstd[:, 1:2], bias=shift[:, 1:2]
                )

            def transpose_pass(tiles):
                z = []
                for half in range(2):
                    z_ps = psum_tr.tile([P, 2, ROWS], F32, name="z_ps", tag="tr")
                    for i in range(2):
                        for m in range(M_TILES):
                            nc.tensor.transpose(z_ps[:, i, m * P : (m + 1) * P], tiles[m][:, 2 * half + i, :], ident[:])
                    z.append(z_ps)
                return z

            def silu_pass(xp, z):
                st, j = streams[xp // HID_BANKS], xp % HID_BANKS
                x_t = xt_pool.tile([P, PACK, ROWS], BF16, name="x_t")
                for t in range(PACK):
                    nc.scalar.activation(
                        out=x_t[:, t, :],
                        in_=z[t // 2][:, t % 2, :],
                        func=ACT.Silu,
                        scale=gain_bias[:, t, st["gain_row"] + j : st["gain_row"] + j + 1],
                        bias=gain_bias[:, t, st["bias_row"] + j : st["bias_row"] + j + 1],
                    )
                return x_t

            def quantise_x(xp, x_grouped):
                k_pass = streams[xp // HID_BANKS]["first_pass"] + xp % HID_BANKS
                nc.vector.quantize_mx(
                    out=x_codes[:, k_pass, :].bitcast(FP8X4),
                    scales=x_planes[:, k_pass, :],
                    in_=x_grouped[:].rearrange("p n t -> p (n t)"),
                )

            def regroup_pair(slot, steps):
                raw = w_raw[slot]
                grouped = w_grouped_pool.tile([P, 2 * BLK, PACK], BF16, name="w_grouped", align_bytes=64)
                v_cols = vector_columns(slot)
                for copy, lo, hi in [(nc.vector.tensor_copy, 0, v_cols), (nc.scalar.copy, v_cols, 2 * BLK)]:
                    for c in range(2):
                        a, b = max(lo, c * BLK), min(hi, (c + 1) * BLK)
                        if a < b:
                            regroup(copy, grouped[:, a:b, :], raw[:, c, :, a - c * BLK : b - c * BLK])
                            if steps and hi == v_cols:
                                steps.pop(0)()
                return grouped

            def quantise_w(slot, grouped, ready):
                codes = w_codes_pool.tile([P, 2, BLK], U32, name="w_codes", align_bytes=64)
                plane = w_codes_pool.tile([P, 2, BLK], U8, name="w_plane", align_bytes=64)
                nc.vector.quantize_mx(
                    out=codes[:].rearrange("p c n -> p (c n)").bitcast(FP8X4),
                    scales=plane[:].rearrange("p c n -> p (c n)"),
                    in_=grouped[:].rearrange("p n t -> p (n t)"),
                )
                for c in range(2):
                    block, pos = pair_place(slot, c)
                    ready.append((codes[:, c, :], plane[:, c, :], block, pos))

            acc = [[psum_acc.tile([P, BANK], F32, name="acc") for m in range(M_TILES)] for block in range(2)]

            multiplied = [0] * BLOCKS

            def multiply_ready(chunks, x_done, banks_free):
                n = 0
                left = []
                for chunk in chunks:
                    codes, plane, block, pos = chunk
                    k_pass = pass_order[pos][0]
                    if n == MAX_PASSES_A_SLOT or pass_order[pos][1] > x_done or (block == 2 and not banks_free):
                        left.append(chunk)
                        continue
                    n = n + 1
                    if block == len(acc):
                        acc.append([psum_h.tile([P, BANK], F32, name="acc_last", tag="h") for m in range(M_TILES)])
                    for m in range(M_TILES):
                        m_cols = slice(m * P, (m + 1) * P)
                        if k_pass == 0:
                            lhs, lhs_plane = in_codes[:, 3 + block, m_cols], in_planes[:, 3 + block, m_cols]
                        else:
                            lhs, lhs_plane = x_codes[:, k_pass - 1, m_cols], x_planes[:, k_pass - 1, m_cols]
                        nc.tensor.matmul_mx(
                            out=acc[block][m][:],
                            lhsT=lhs.bitcast(FP8X4),
                            lhsT_scale=lhs_plane,
                            rhs=codes.bitcast(FP8X4),
                            rhs_scale=plane,
                            start=(multiplied[block] == 0),
                            stop=(multiplied[block] == HID_PASSES - 1),
                        )
                    multiplied[block] = multiplied[block] + 1
                    if multiplied[block] == HID_PASSES:
                        for m in range(M_TILES):
                            nc.vector.bn_stats(out=out_stats[m][:, block, :], in_=acc[block][m][:])
                return left

            banks = None
            u_tiles = []
            sums = None
            neg_first = None
            scalars = []
            z = []
            x_t = None
            waiting = []
            ready = []
            x_done = 0
            for t in range(N_SLOTS):
                e = t - X_START
                xp = e - X_LAG

                steps = []
                if e % HID_BANKS == 0 and 0 < e <= X_PASSES:
                    steps, rstd, shift = stream_scalars(sums, neg_first)
                    scalars.append((rstd, shift))

                x_t_before = x_t
                if e in late_groups:
                    in_grouped = transpose_input(late_groups[e][0], late_groups[e][1])
                if 0 <= xp < X_PASSES:
                    z = transpose_pass(u_tiles[xp])
                if 0 <= e < X_PASSES:
                    if e % HID_BANKS == 0:
                        sums = small.tile([P, 2, M_TILES, HID_BANKS], F32, name="sums")
                    u_tiles.append(copy_out(banks, sums, e % HID_BANKS))
                    if e % HID_BANKS == HID_BANKS - 1:
                        sum_squares(u_tiles[e], sums, neg_first, e % HID_BANKS)

                if e == 3:
                    vec_sorted = sort_gains()
                if e == 4:
                    gb_ps = transpose_gains(vec_sorted)
                if e == 5:
                    nc.vector.tensor_copy(out=gain_bias[:], in_=gb_ps[:])

                ready = multiply_ready(ready, x_done, e >= X_PASSES)

                if steps:
                    steps.pop(0)()
                    if x_t_before is None:
                        steps.pop(0)()
                if t < N_PAIRS:
                    waiting.append((t, regroup_pair(t, steps)))
                if 0 <= e < X_PASSES and e % HID_BANKS == 0:
                    neg_first = first_means(sums)
                load_for(t + AHEAD)

                x_t = silu_pass(xp, z) if 0 <= xp < X_PASSES else None

                if x_t_before is not None:
                    x_grouped = xt_pool.tile([P, ROWS, PACK], BF16, name="x_grouped", align_bytes=64)
                    regroup(nc.vector.tensor_copy, x_grouped[:], x_t_before[:])
                    if steps:
                        steps.pop(0)()
                if waiting and waiting[0][0] <= t - W_LAG:
                    quantise_w(waiting[0][0], waiting[0][1], ready)
                    waiting = waiting[1:]
                    if steps:
                        steps.pop(0)()
                if 0 <= e < X_PASSES and e % HID_BANKS != HID_BANKS - 1:
                    sum_squares(u_tiles[e], sums, neg_first, e % HID_BANKS)
                if x_t_before is not None:
                    quantise_x(xp - 1, x_grouped)
                    x_done = x_done + 1
                for step in steps:
                    step()
                if e in late_groups:
                    quantise_input(late_groups[e][0], late_groups[e][1], in_grouped)
                if t == N_PAIRS - AHEAD:
                    nc.sync.dma_start(out=out_gain_bias[:, 0:DETER], in_=ln_h_g.partition_broadcast(P))
                    nc.sync.dma_start(out=out_gain_bias[:, DETER:], in_=ln_h_b.partition_broadcast(P))

                xn = xp + 1
                if 0 <= xn < X_PASSES:
                    normalise(u_tiles[xn], scalars[xn // HID_BANKS][0], scalars[xn // HID_BANKS][1])
                if 0 <= e + 1 < X_PASSES:
                    banks = embed(e + 1)

            for slot, grouped in waiting:
                quantise_w(slot, grouped, ready)
            while ready:
                ready = multiply_ready(ready, x_done, True)

        with tc.tile_pool(name="final", bufs=6) as final:
            mean_var = small.tile([P, M_TILES, 2], F32, name="mean_var")
            for m in range(M_TILES):
                nc.vector.bn_aggr(out=mean_var[:, m, :], in_=out_stats[m][:].rearrange("p a b -> p (a b)"))
            units = [(m, g) for m in range(M_TILES) for g in range(BLOCKS)]
            centred = []

            def centre():
                m, g = units[len(centred)]
                c_tile = final.tile([P, BLK], F32, name="centred")
                nc.vector.scalar_tensor_tensor(
                    out=c_tile[:], in0=acc[g][m][:], scalar=mean_var[:, m, 0:1],
                    in1=out_gain_bias[:, g * BLK : (g + 1) * BLK], op0=ALU.subtract, op1=ALU.mult,
                )
                centred.append(c_tile)

            z_banks = []
            for n in range(1):
                bank = psum_tr.tile([P, BLK], F32, name="z_bank", tag="tr")
                g = units[n][1]
                nc.tensor.matmul(
                    bank[:], ident_bf[:], out_gain_bias[:, DETER + g * BLK : DETER + (g + 1) * BLK], start=True, stop=False
                )
                z_banks.append(bank)

            centre()
            var_eps = small.tile([P, M_TILES], F32, name="var_eps")
            nc.vector.tensor_scalar_add(out=var_eps[:], in0=mean_var[:, :, 1], scalar1=EPS)
            rstd = small.tile([P, M_TILES], F32, name="rstd")
            nc.gpsimd.tensor_tensor(out=rstd[:], in0=var_eps[:], in1=neg_half[:], op=ALU.pow)
            diagonal = final.tile([P, P], F32, name="diagonal")
            nc.scalar.activation(out=diagonal[:], in_=ident[:], func=ACT.Copy, scale=rstd[:, 0:1])
            for n in range(1, 1):
                centre()
            for n in range(1):
                nc.tensor.matmul(z_banks[n][:], diagonal[:], centred[n][:], start=False, stop=True)

            def finish(n, z):
                m, g = units[n]
                result = final.tile([P, BLK], F32, name="result")
                nc.scalar.activation(out=result[:], in_=z, func=ACT.Silu)
                nc.sync.dma_start(out=out[m * P : (m + 1) * P, g * BLK : (g + 1) * BLK], in_=result[:])

            centre()
            for n in range(1, len(units)):
                if len(centred) < len(units):
                    centre()
                m, g = units[n]
                z_tile = final.tile([P, BLK], F32, name="z")
                nc.vector.scalar_tensor_tensor(
                    out=z_tile[:], in0=centred[n][:], scalar=rstd[:, m : m + 1],
                    in1=out_gain_bias[:, DETER + g * BLK : DETER + (g + 1) * BLK], op0=ALU.mult, op1=ALU.add,
                )
                finish(n, z_tile[:])
                if n == 2:
                    finish(0, z_banks[0][:])
